import numpy as np
import ml_dtypes


def mxq(x, axis, fmt="e4m3"):
    dtype, down = {"e4m3": (ml_dtypes.float8_e4m3fn, 7), "e5m2": (ml_dtypes.float8_e5m2, 14)}[fmt]
    v = np.moveaxis(np.asarray(x, np.float32).astype(ml_dtypes.bfloat16).astype(np.float64), axis, -1)
    blocks = v.reshape(v.shape[:-1] + (-1, 32))
    amax = np.abs(blocks).max(-1, keepdims=True)
    byte = np.maximum(np.where(amax > 0, np.frexp(amax)[1] - 1 + 127, 0) - down, 1)
    scale = np.exp2(byte - 127.0)
    codes = (blocks / scale).astype(np.float32).astype(dtype).astype(np.float64)
    return np.moveaxis((codes * scale).reshape(v.shape), -1, axis)


BF16 = ml_dtypes.bfloat16


def bf(x):
    return np.asarray(x, np.float32).astype(BF16)


def f64(x):
    return np.asarray(x).astype(np.float64)


N1, N2, D, R = 8192, 128, 1024, 4
NDUP = N2 // 4
SQRT3 = np.sqrt(3.0)


def setup_inputs():
    c = 0.35 / np.sqrt(D)
    p = np.random.standard_normal((R, D))
    mu = 10.0 * np.random.standard_normal(D)
    x1 = bf((mu + np.random.standard_normal((N1, R)) @ p + np.random.standard_normal((N1, D))) * c)
    x2 = bf((mu + np.random.standard_normal((N2, R)) @ p + np.random.standard_normal((N2, D))) * c)
    x2[:NDUP] = x1[:NDUP]
    lengthscale = bf(np.exp(0.3 * np.random.standard_normal(D)))
    return {"x1": x1, "x2": x2, "lengthscale": lengthscale}


def reference(x1, x2, lengthscale):
    x1, x2, lengthscale = f64(x1), f64(x2), f64(lengthscale)
    adjustment = np.mean(x1, axis=-2, keepdims=True)
    x1_ = (x1 - adjustment) / lengthscale
    x2_ = (x2 - adjustment) / lengthscale
    sq1 = np.sum(x1_ * x1_, axis=-1, keepdims=True)
    sq2 = np.sum(x2_ * x2_, axis=-1)
    d2 = sq1 + sq2[None, :] - 2.0 * (mxq(x1_, 1, "e4m3") @ mxq(x2_, 1, "e4m3").T)
    distance = np.sqrt(np.maximum(d2, 0.0))
    distance = np.maximum(distance, 1e-15)
    return (1.0 + SQRT3 * distance) * np.exp(-SQRT3 * distance)

@@ -1,0 +1,292 @@
+from contextlib import ExitStack
+
+import concourse.mybir as mybir
+from concourse.masks import make_identity
+
+FLOPS = 2 * 8192 * 128 * 1024
+
+MANUAL = True
+E1S = (2, 1)
+BATCH = (5, 5, 4, 2)
+
+FP8X4 = mybir.dt.float8_e4m3fn_x4
+BF16 = mybir.dt.bfloat16
+F32 = mybir.dt.float32
+U32 = mybir.dt.uint32
+U8 = mybir.dt.uint8
+ALU = mybir.AluOpType
+ACT = mybir.ActivationFunctionType
+AX = mybir.AxisListType
+
+P = 128
+N1 = 8192
+D = 1024
+NT = N1 // P
+CH = 8
+NCH = NT // CH
+GW = 512
+NG = N1 // GW
+
+
+def tile_maternkernel_t_kernel(tc, x1, x2, lengthscale, out):
+    nc = tc.nc
+    x1v = x1.rearrange("(p t) f -> p t f", t=NT)
+    outv = out.rearrange("(p t) n -> p t n", t=NT)
+    with ExitStack() as ctx:
+        if MANUAL:
+            ctx.enter_context(tc.manual_schedule())
+        const = ctx.enter_context(tc.tile_pool(name="const", bufs=1))
+        work = ctx.enter_context(tc.tile_pool(name="work", bufs=2))
+        ps1 = ctx.enter_context(tc.psum_pool(name="ps1", bufs=3))
+        ps2 = ctx.enter_context(tc.psum_pool(name="ps2", bufs=3))
+        psm = ctx.enter_context(tc.psum_pool(name="psm", bufs=2))
+
+        lsz = const.tile([P, P], BF16, name="lsz")
+        nc.vector.memset(lsz[:], 0.0)
+        nc.scalar.dma_start(out=lsz[0:8, :], in_=lengthscale.rearrange("(k p) -> k p", p=P))
+        x2n = const.tile([P, D], BF16, name="x2n")
+        nc.scalar.dma_start(out=x2n[:], in_=x2)
+
+        xn = {}
+
+        def load(q):
+            h, c = q // NCH, q % NCH
+            t = work.tile([P, CH, 512], BF16, name="xn", tag="xn", bufs=3)
+            nc.sync.dma_start(out=t[:], in_=x1v[:, c * CH:(c + 1) * CH, h * 512:(h + 1) * 512])
+            xn[q] = t
+
+        for q in range(3):
+            load(q)
+
+        identb = const.tile([P, P], BF16, name="identb")
+        make_identity(nc, identb[:])
+        identf = const.tile([P, P], F32, name="identf")
+        make_identity(nc, identf[:])
+        ones = const.tile([P, P], F32, name="ones")
+        nc.vector.memset(ones[:], 1.0)
+        warm = const.tile([P, 1], F32, name="warm")
+        nc.scalar.activation(out=warm[:], in_=ones[:, 0:1], func=ACT.Sqrt)
+
+        lsT = const.tile([P, 8], F32, name="lsT")
+        rls = const.tile([P, 8], F32, name="rls")
+        x2T = const.tile([P, 8, P], BF16, name="x2T")
+
+        def small_inputs():
+            pl = ps1.tile([P, 1024], BF16, name="pl", tag="pt")
+            nc.tensor.transpose(pl[:, 0:P], lsz[:], identb[:])
+            nc.vector.tensor_copy(out=lsT[:], in_=pl[:, 0:8])
+            nc.vector.reciprocal(out=rls[:], in_=lsT[:])
+            px = ps1.tile([P, 1024], BF16, name="px", tag="pt")
+            for kt in range(8):
+                nc.tensor.transpose(px[:, kt * P:(kt + 1) * P], x2n[:, kt * P:(kt + 1) * P], identb[:])
+            nc.vector.tensor_copy(out=x2T[:].rearrange("p k n -> p (k n)"), in_=px[:])
+
+        codes0 = const.tile([P, N1], U32, name="codes0", align_bytes=64)
+        scales0 = const.tile([P, N1], U8, name="scales0", align_bytes=64)
+        bcodes = [const.tile([P, P], U32, name="bcodes%d" % h, align_bytes=64) for h in range(2)]
+        bscales = [const.tile([P, P], U8, name="bscales%d" % h, align_bytes=64) for h in range(2)]
+        sqp = [const.tile([P, NT], F32, name="sqp%d" % h) for h in range(2)]
+        sq2p = const.tile([P, 2], F32, name="sq2p")
+        sq2bc = const.tile([P, P], F32, name="sq2bc")
+        sumsV = [const.tile([P, 4 - E1S[h], NCH], F32, name="sumsV%d" % h) for h in range(2)]
+        sumsS = [const.tile([P, E1S[h], NCH], F32, name="sumsS%d" % h) for h in range(2)]
+        mean = [const.tile([P, 4], F32, name="mean%d" % h) for h in range(2)]
+        nbias = [const.tile([P, 4], F32, name="nbias%d" % h) for h in range(2)]
+
+        xT = {}
+
+        def unit(h, u):
+            c, j = u // 4, u % 4
+            q = h * NCH + c
+            if j == 0:
+                xT[q] = work.tile([P, 4, CH * P], BF16, name="xT", tag="xT", bufs=10)
+            pt = ps1.tile([P, 1024], BF16, name="pt", tag="pt")
+            for tt in range(CH):
+                nc.tensor.transpose(pt[:, tt * P:(tt + 1) * P], xn[q][:, tt, j * P:(j + 1) * P], identb[:])
+            nv = 4 - E1S[h]
+            if j < nv:
+                nc.vector.tensor_scalar(out=xT[q][:, j, :], in0=pt[:], scalar1=1.0, scalar2=None,
+                                        op0=ALU.mult, op1=ALU.add, accum_out=sumsV[h][:, j, c:c + 1])
+            else:
+                nc.scalar.activation(out=xT[q][:, j, :], in_=pt[:], func=ACT.Copy,
+                                     accum_out=sumsS[h][:, j - nv, c:c + 1])
+            if j == 3 and q + 3 < 2 * NCH:
+                load(q + 3)
+
+        def mean_of(h):
+            nv = 4 - E1S[h]
+            msum = const.tile([P, 4], F32, name="msum%d" % h)
+            nc.vector.tensor_reduce(out=msum[:, 0:nv], in_=sumsV[h][:], axis=AX.X, op=ALU.add)
+            nc.vector.tensor_reduce(out=msum[:, nv:4], in_=sumsS[h][:], axis=AX.X, op=ALU.add)
+            nc.vector.tensor_scalar(out=mean[h][:], in0=msum[:], scalar1=1.0 / N1, scalar2=None, op0=ALU.mult)
+            nc.vector.scalar_tensor_tensor(out=nbias[h][:], in0=mean[h][:], scalar=-1.0,
+                                           in1=rls[:, 4 * h:4 * h + 4], op0=ALU.mult, op1=ALU.mult)
+
+        def affine(h, j, dst, src):
+            nc.vector.tensor_scalar(out=dst, in0=src, scalar1=mean[h][:, j:j + 1],
+                                    scalar2=rls[:, 4 * h + j:4 * h + j + 1], op0=ALU.subtract, op1=ALU.mult)
+
+        def square(h, j, dst, src):
+            nc.scalar.activation(out=dst, in_=src, func=ACT.Square, bias=nbias[h][:, j:j + 1],
+                                 scale=rls[:, 4 * h + j:4 * h + j + 1])
+
+        def bpost(h):
+            abb = const.tile([P, 4, P], BF16, name="abb%d" % h)
+            sqb = const.tile([P, 4, P], F32, name="sqb%d" % h)
+            for j in range(4):
+                square(h, j, sqb[:, j, :], x2T[:, 4 * h + j, :])
+                affine(h, j, abb[:, j, :], x2T[:, 4 * h + j, :])
+            grb = const.tile([P, P, 4], BF16, name="grb%d" % h, align_bytes=64)
+            nc.vector.tensor_copy(out=grb[:], in_=abb[:].rearrange("p j r -> p r j"))
+            nc.vector.quantize_mx(out=bcodes[h][:].bitcast(FP8X4), scales=bscales[h][:],
+                                  in_=grb[:].rearrange("p r j -> p (r j)"))
+            pb = ps2.tile([P, 512], F32, name="pb", tag="pa")
+            for j in range(4):
+                nc.tensor.matmul(out=pb[:, 0:P], lhsT=sqb[:, j, :], rhs=identf[:], is_transpose=True,
+                                 start=(j == 0), stop=(j == 3))
+            nc.vector.tensor_reduce(out=sq2p[:, h:h + 1], in_=pb[:, 0:P], axis=AX.X, op=ALU.add)
+
+        def sq2_spread():
+            sq2 = const.tile([P, 1], F32, name="sq2")
+            nc.vector.tensor_reduce(out=sq2[:], in_=sq2p[:], axis=AX.X, op=ALU.add)
+            rep = const.tile([P, P], F32, name="rep")
+            nc.vector.tensor_scalar(out=rep[:], in0=ones[:], scalar1=sq2[:, 0:1], scalar2=None, op0=ALU.mult)
+            pr = ps2.tile([P, 512], F32, name="pr", tag="pa")
+            nc.tensor.transpose(pr[:, 0:P], rep[:], identf[:])
+            nc.vector.tensor_copy(out=sq2bc[:], in_=pr[:, 0:P])
+
+        sq = {}
+        ab = {}
+        gr = {}
+        pa = {}
+        cod = {}
+        sca = {}
+        pm = {}
+        wt = {}
+        et = {}
+
+        def src_of(k, j):
+            h, g = k // NG, k % NG
+            return xT[h * NCH + g // 2][:, j, (g % 2) * GW:(g % 2 + 1) * GW]
+
+        def st_square(k):
+            sq[k] = work.tile([P, 4, GW], F32, name="sq", tag="sq", bufs=2)
+            for j in range(4):
+                square(k // NG, j, sq[k][:, j, :], src_of(k, j))
+
+        def st_affine(k):
+            ab[k] = work.tile([P, 4, GW], BF16, name="ab", tag="ab", bufs=2)
+            for j in range(4):
+                affine(k // NG, j, ab[k][:, j, :], src_of(k, j))
+
+        def st_group(k):
+            gr[k] = work.tile([P, GW, 4], BF16, name="gr", tag="gr", bufs=2, align_bytes=64)
+            nc.vector.tensor_copy(out=gr[k][:], in_=ab[k][:].rearrange("p j r -> p r j"))
+
+        def st_quant(k):
+            h, g = k // NG, k % NG
+            if h == 0:
+                cod[k] = codes0[:, g * GW:(g + 1) * GW]
+                sca[k] = scales0[:, g * GW:(g + 1) * GW]
+            else:
+                c1 = work.tile([P, GW], U32, name="c1", tag="c1", bufs=4, align_bytes=64)
+                s1 = work.tile([P, GW], U8, name="s1", tag="s1", bufs=4, align_bytes=64)
+                cod[k] = c1[:]
+                sca[k] = s1[:]
+            nc.vector.quantize_mx(out=cod[k].bitcast(FP8X4), scales=sca[k],
+                                  in_=gr[k][:].rearrange("p r j -> p (r j)"))
+
+        def st_t2(k):
+            pa[k] = ps2.tile([P, 512], F32, name="pa", tag="pa")
+            for tl in range(4):
+                for j in range(4):
+                    nc.tensor.matmul(out=pa[k][:, tl * P:(tl + 1) * P], lhsT=sq[k][:, j, tl * P:(tl + 1) * P],
+                                     rhs=identf[:], is_transpose=True, start=(j == 0), stop=(j == 3))
+
+        def st_red(k):
+            h, g = k // NG, k % NG
+            nc.vector.tensor_reduce(out=sqp[h][:, 4 * g:4 * g + 4],
+                                    in_=pa[k][:].rearrange("p (t n) -> p t n", n=P), axis=AX.X, op=ALU.add)
+
+        def st_mx(g):
+            pm[g] = psm.tile([P, 512], F32, name="pm", tag="pm")
+            for tl in range(4):
+                for h in range(2):
+                    k = h * NG + g
+                    nc.tensor.matmul_mx(out=pm[g][:, tl * P:(tl + 1) * P],
+                                        lhsT=cod[k][:, tl * P:(tl + 1) * P].bitcast(FP8X4),
+                                        lhsT_scale=sca[k][:, tl * P:(tl + 1) * P],
+                                        rhs=bcodes[h][:].bitcast(FP8X4), rhs_scale=bscales[h][:],
+                                        start=(h == 0), stop=(h == 1))
+
+        def st_d2(g):
+            sq1g = work.tile([P, 4], F32, name="sq1g", tag="sq1g", bufs=3)
+            nc.vector.tensor_tensor(out=sq1g[:], in0=sqp[0][:, 4 * g:4 * g + 4], in1=sqp[1][:, 4 * g:4 * g + 4],
+                                    op=ALU.add)
+            wt[g] = work.tile([P, 4, P], F32, name="wt", tag="wt", bufs=8)
+            nc.vector.scalar_tensor_tensor(out=wt[g][:], in0=pm[g][:].rearrange("p (t n) -> p t n", n=P),
+                                           scalar=-2.0, in1=sq2bc[:].unsqueeze(1).to_broadcast([P, 4, P]),
+                                           op0=ALU.mult, op1=ALU.add)
+            for tl in range(4):
+                nc.vector.tensor_scalar(out=wt[g][:, tl, :], in0=wt[g][:, tl, :], scalar1=sq1g[:, tl:tl + 1],
+                                        scalar2=1e-30, op0=ALU.add, op1=ALU.max)
+
+        def st_sqrt(g):
+            nc.scalar.activation(out=wt[g][:], in_=wt[g][:], func=ACT.Sqrt, scale=3.0)
+
+        def st_exp(g):
+            et[g] = work.tile([P, 4, P], F32, name="et", tag="et", bufs=5)
+            nc.scalar.activation(out=et[g][:], in_=wt[g][:], func=ACT.Exp, scale=-1.0)
+
+        def st_out(g):
+            nc.vector.scalar_tensor_tensor(out=et[g][:], in0=wt[g][:], scalar=1.0, in1=et[g][:],
+                                           op0=ALU.add, op1=ALU.mult)
+            nc.sync.dma_start(out=outv[:, 4 * g:4 * g + 4, :], in_=et[g][:])
+
+        batch_of = {}
+        g0 = 0
+        for b in BATCH:
+            batch_of[g0 + b - 1] = list(range(g0, g0 + b))
+            g0 += b
+
+        for u in range(4 * NCH):
+            unit(0, u)
+            if u == 11:
+                small_inputs()
+        mean_of(0)
+        bpost(0)
+
+        pending = []
+        for s in range(2 * NG + 8):
+            if s < NG:
+                unit(1, 2 * s)
+                unit(1, 2 * s + 1)
+            if 0 <= s - 1 < 2 * NG:
+                st_quant(s - 1)
+                st_t2(s - 1)
+            if s == NG:
+                mean_of(1)
+                bpost(1)
+                sq2_spread()
+            todo = pending
+            pending = []
+            gs = s - NG - 4
+            if 0 <= gs < NG:
+                st_sqrt(gs)
+                if gs in batch_of:
+                    for g in batch_of[gs]:
+                        st_exp(g)
+                    pending = batch_of[gs]
+            if s < 2 * NG:
+                st_square(s)
+                st_affine(s)
+            if 0 <= s - 2 < 2 * NG:
+                st_red(s - 2)
+            if s < 2 * NG:
+                st_group(s)
+            if 0 <= s - NG - 2 < NG:
+                st_mx(s - NG - 2)
+            if 0 <= s - NG - 3 < NG:
+                st_d2(s - NG - 3)
+            for g in todo:
+                st_out(g)

@@ -8,6 +8,8 @@ FLOPS = 2 * 8192 * 128 * 1024
 MANUAL = True
 E1S = (2, 1)
 BATCH = (5, 5, 4, 2)
+WARM = 6
+IDLE = 2
 
 FP8X4 = mybir.dt.float8_e4m3fn_x4
 BF16 = mybir.dt.bfloat16
@@ -38,9 +40,23 @@ def tile_maternkernel_t_kernel(tc, x1, x2, lengthscale, out):
         const = ctx.enter_context(tc.tile_pool(name="const", bufs=1))
         work = ctx.enter_context(tc.tile_pool(name="work", bufs=2))
         ps1 = ctx.enter_context(tc.psum_pool(name="ps1", bufs=3))
-        ps2 = ctx.enter_context(tc.psum_pool(name="ps2", bufs=3))
+        ps2 = ctx.enter_context(tc.psum_pool(name="ps2", bufs=2))
+        psd = ctx.enter_context(tc.psum_pool(name="psd", bufs=1))
         psm = ctx.enter_context(tc.psum_pool(name="psm", bufs=2))
 
+        zb = const.tile([P, 2048], BF16, name="zb", align_bytes=64)
+        nc.vector.memset(zb[:], 1.0)
+        zc = const.tile([P, 512], U32, name="zc", align_bytes=64)
+        zs = const.tile([P, 512], U8, name="zs", align_bytes=64)
+        nc.vector.quantize_mx(out=zc[:].bitcast(FP8X4), scales=zs[:], in_=zb[:])
+        pd = psd.tile([P, 512], F32, name="pd")
+
+        def idle_passes(n):
+            for i in range(n):
+                nc.tensor.matmul_mx(out=pd[:], lhsT=zc[:, 0:P].bitcast(FP8X4), lhsT_scale=zs[:, 0:P],
+                                    rhs=zc[:].bitcast(FP8X4), rhs_scale=zs[:], start=True, stop=True)
+
+        idle_passes(WARM)
         lsz = const.tile([P, P], BF16, name="lsz")
         nc.vector.memset(lsz[:], 0.0)
         nc.scalar.dma_start(out=lsz[0:8, :], in_=lengthscale.rearrange("(k p) -> k p", p=P))
@@ -110,6 +126,8 @@ def tile_maternkernel_t_kernel(tc, x1, x2, lengthscale, out):
             else:
                 nc.scalar.activation(out=xT[q][:, j, :], in_=pt[:], func=ACT.Copy,
                                      accum_out=sumsS[h][:, j - nv, c:c + 1])
+            if j % 2 == 1:
+                idle_passes(IDLE)
             if j == 3 and q + 3 < 2 * NCH:
                 load(q + 3)
 
@@ -140,7 +158,7 @@ def tile_maternkernel_t_kernel(tc, x1, x2, lengthscale, out):
             nc.vector.tensor_copy(out=grb[:], in_=abb[:].rearrange("p j r -> p r j"))
             nc.vector.quantize_mx(out=bcodes[h][:].bitcast(FP8X4), scales=bscales[h][:],
                                   in_=grb[:].rearrange("p r j -> p (r j)"))
-            pb = ps2.tile([P, 512], F32, name="pb", tag="pa")
+            pb = psm.tile([P, 512], F32, name="pb", tag="pm")
             for j in range(4):
                 nc.tensor.matmul(out=pb[:, 0:P], lhsT=sqb[:, j, :], rhs=identf[:], is_transpose=True,
                                  start=(j == 0), stop=(j == 3))
@@ -151,7 +169,7 @@ def tile_maternkernel_t_kernel(tc, x1, x2, lengthscale, out):
             nc.vector.tensor_reduce(out=sq2[:], in_=sq2p[:], axis=AX.X, op=ALU.add)
             rep = const.tile([P, P], F32, name="rep")
             nc.vector.tensor_scalar(out=rep[:], in0=ones[:], scalar1=sq2[:, 0:1], scalar2=None, op0=ALU.mult)
-            pr = ps2.tile([P, 512], F32, name="pr", tag="pa")
+            pr = psm.tile([P, 512], F32, name="pr", tag="pm")
             nc.tensor.transpose(pr[:, 0:P], rep[:], identf[:])
             nc.vector.tensor_copy(out=sq2bc[:], in_=pr[:, 0:P])
 
@@ -202,6 +220,7 @@ def tile_maternkernel_t_kernel(tc, x1, x2, lengthscale, out):
                 for j in range(4):
                     nc.tensor.matmul(out=pa[k][:, tl * P:(tl + 1) * P], lhsT=sq[k][:, j, tl * P:(tl + 1) * P],
                                      rhs=identf[:], is_transpose=True, start=(j == 0), stop=(j == 3))
+            idle_passes(IDLE)
 
         def st_red(k):
             h, g = k // NG, k % NG

@@ -6,10 +6,13 @@ from concourse.masks import make_identity
 FLOPS = 2 * 8192 * 128 * 1024
 
 MANUAL = True
-E1S = (2, 1)
+E1S = (1, 1)
 BATCH = (5, 5, 4, 2)
+PLAIN = True
+XNB = 3
+XTB = 10
 WARM = 6
-IDLE = 2
+IDLE = (2, 2, 1, 1)
 
 FP8X4 = mybir.dt.float8_e4m3fn_x4
 BF16 = mybir.dt.bfloat16
@@ -67,11 +70,11 @@ def tile_maternkernel_t_kernel(tc, x1, x2, lengthscale, out):
 
         def load(q):
             h, c = q // NCH, q % NCH
-            t = work.tile([P, CH, 512], BF16, name="xn", tag="xn", bufs=3)
+            t = work.tile([P, CH, 512], BF16, name="xn", tag="xn", bufs=XNB)
             nc.sync.dma_start(out=t[:], in_=x1v[:, c * CH:(c + 1) * CH, h * 512:(h + 1) * 512])
             xn[q] = t
 
-        for q in range(3):
+        for q in range(XNB):
             load(q)
 
         identb = const.tile([P, P], BF16, name="identb")
@@ -115,7 +118,7 @@ def tile_maternkernel_t_kernel(tc, x1, x2, lengthscale, out):
             c, j = u // 4, u % 4
             q = h * NCH + c
             if j == 0:
-                xT[q] = work.tile([P, 4, CH * P], BF16, name="xT", tag="xT", bufs=10)
+                xT[q] = work.tile([P, 4, CH * P], BF16, name="xT", tag="xT", bufs=XTB)
             pt = ps1.tile([P, 1024], BF16, name="pt", tag="pt")
             for tt in range(CH):
                 nc.tensor.transpose(pt[:, tt * P:(tt + 1) * P], xn[q][:, tt, j * P:(j + 1) * P], identb[:])
@@ -127,9 +130,13 @@ def tile_maternkernel_t_kernel(tc, x1, x2, lengthscale, out):
                 nc.scalar.activation(out=xT[q][:, j, :], in_=pt[:], func=ACT.Copy,
                                      accum_out=sumsS[h][:, j - nv, c:c + 1])
             if j % 2 == 1:
-                idle_passes(IDLE)
-            if j == 3 and q + 3 < 2 * NCH:
-                load(q + 3)
+                if h == 0 and PLAIN:
+                    for i in range(IDLE[h]):
+                        nc.tensor.matmul(out=pd[:, 0:P], lhsT=identf[:], rhs=identf[:], start=True, stop=True)
+                else:
+                    idle_passes(IDLE[h])
+            if j == 3 and q + XNB < 2 * NCH:
+                load(q + XNB)
 
         def mean_of(h):
             nv = 4 - E1S[h]
@@ -199,7 +206,8 @@ def tile_maternkernel_t_kernel(tc, x1, x2, lengthscale, out):
 
         def st_group(k):
             gr[k] = work.tile([P, GW, 4], BF16, name="gr", tag="gr", bufs=2, align_bytes=64)
-            nc.vector.tensor_copy(out=gr[k][:], in_=ab[k][:].rearrange("p j r -> p r j"))
+            nc.vector.tensor_copy(out=gr[k][:].rearrange("p (c i) t -> p c t i", i=4),
+                                  in_=ab[k][:].rearrange("p t (c i) -> p c t i", i=4))
 
         def st_quant(k):
             h, g = k // NG, k % NG
@@ -220,7 +228,7 @@ def tile_maternkernel_t_kernel(tc, x1, x2, lengthscale, out):
                 for j in range(4):
                     nc.tensor.matmul(out=pa[k][:, tl * P:(tl + 1) * P], lhsT=sq[k][:, j, tl * P:(tl + 1) * P],
                                      rhs=identf[:], is_transpose=True, start=(j == 0), stop=(j == 3))
-            idle_passes(IDLE)
+            idle_passes(IDLE[2 + k // NG])
 
         def st_red(k):
             h, g = k // NG, k % NG

@@ -5,7 +5,7 @@ from concourse.masks import make_identity
 
 FLOPS = 2 * 8192 * 128 * 1024
 
-MANUAL = True
+MANUAL = False
 E1S = (1, 1)
 BATCH = (5, 5, 4, 2)
 PLAIN = True

@@ -8,11 +8,10 @@ FLOPS = 2 * 8192 * 128 * 1024
 MANUAL = False
 E1S = (1, 1)
 BATCH = (5, 5, 4, 2)
+EVERY = 4
 PLAIN = True
-XNB = 3
-XTB = 10
 WARM = 6
-IDLE = (2, 2, 1, 1)
+IDLE = (2, 2, 2, 1)
 
 FP8X4 = mybir.dt.float8_e4m3fn_x4
 BF16 = mybir.dt.bfloat16
@@ -42,6 +41,7 @@ def tile_maternkernel_t_kernel(tc, x1, x2, lengthscale, out):
             ctx.enter_context(tc.manual_schedule())
         const = ctx.enter_context(tc.tile_pool(name="const", bufs=1))
         work = ctx.enter_context(tc.tile_pool(name="work", bufs=2))
+        big = ctx.enter_context(tc.tile_pool(name="big", bufs=1))
         ps1 = ctx.enter_context(tc.psum_pool(name="ps1", bufs=3))
         ps2 = ctx.enter_context(tc.psum_pool(name="ps2", bufs=2))
         psd = ctx.enter_context(tc.psum_pool(name="psd", bufs=1))
@@ -70,11 +70,17 @@ def tile_maternkernel_t_kernel(tc, x1, x2, lengthscale, out):
 
         def load(q):
             h, c = q // NCH, q % NCH
-            t = work.tile([P, CH, 512], BF16, name="xn", tag="xn", bufs=XNB)
+            if h == 0:
+                slot = 8 + c % 3
+            elif c < 3:
+                slot = 8 + (c + 2) % 3
+            else:
+                slot = c - 3
+            t = big.tile([P, CH, 512], BF16, name="xn", tag="s%d" % slot)
             nc.sync.dma_start(out=t[:], in_=x1v[:, c * CH:(c + 1) * CH, h * 512:(h + 1) * 512])
             xn[q] = t
 
-        for q in range(XNB):
+        for q in range(3):
             load(q)
 
         identb = const.tile([P, P], BF16, name="identb")
@@ -107,8 +113,8 @@ def tile_maternkernel_t_kernel(tc, x1, x2, lengthscale, out):
         sqp = [const.tile([P, NT], F32, name="sqp%d" % h) for h in range(2)]
         sq2p = const.tile([P, 2], F32, name="sq2p")
         sq2bc = const.tile([P, P], F32, name="sq2bc")
-        sumsV = [const.tile([P, 4 - E1S[h], NCH], F32, name="sumsV%d" % h) for h in range(2)]
-        sumsS = [const.tile([P, E1S[h], NCH], F32, name="sumsS%d" % h) for h in range(2)]
+        sumsV = [const.tile([P, 4 - E1S[h], NCH], F32, name="sumsV%d" % h) for h in range(1)]
+        sumsS = [const.tile([P, E1S[h], NCH], F32, name="sumsS%d" % h) for h in range(1)]
         mean = [const.tile([P, 4], F32, name="mean%d" % h) for h in range(2)]
         nbias = [const.tile([P, 4], F32, name="nbias%d" % h) for h in range(2)]
 
@@ -118,7 +124,7 @@ def tile_maternkernel_t_kernel(tc, x1, x2, lengthscale, out):
             c, j = u // 4, u % 4
             q = h * NCH + c
             if j == 0:
-                xT[q] = work.tile([P, 4, CH * P], BF16, name="xT", tag="xT", bufs=XTB)
+                xT[q] = big.tile([P, 4, CH * P], BF16, name="xT", tag="s%d" % c)
             pt = ps1.tile([P, 1024], BF16, name="pt", tag="pt")
             for tt in range(CH):
                 nc.tensor.transpose(pt[:, tt * P:(tt + 1) * P], xn[q][:, tt, j * P:(j + 1) * P], identb[:])
@@ -129,20 +135,44 @@ def tile_maternkernel_t_kernel(tc, x1, x2, lengthscale, out):
             else:
                 nc.scalar.activation(out=xT[q][:, j, :], in_=pt[:], func=ACT.Copy,
                                      accum_out=sumsS[h][:, j - nv, c:c + 1])
-            if j % 2 == 1:
+            if h == 0 and PLAIN and EVERY == 4:
+                if j == 3:
+                    for i in range(IDLE[h]):
+                        nc.tensor.matmul(out=pd[:, 0:P], lhsT=identf[:], rhs=identf[:], start=True, stop=True)
+            elif j % 2 == 1:
                 if h == 0 and PLAIN:
                     for i in range(IDLE[h]):
                         nc.tensor.matmul(out=pd[:, 0:P], lhsT=identf[:], rhs=identf[:], start=True, stop=True)
                 else:
                     idle_passes(IDLE[h])
-            if j == 3 and q + XNB < 2 * NCH:
-                load(q + XNB)
+            if j == 3 and q + 3 < NCH + 3:
+                load(q + 3)
+
+        onesb = const.tile([P, 2], BF16, name="onesb")
+        nc.vector.memset(onesb[:], 1.0)
+        sums1 = const.tile([P, NCH, 4], F32, name="sums1")
+        pcs = {}
+
+        def col_sums(c):
+            pc = psm.tile([P, 512], F32, name="pc", tag="pm")
+            pcs[c] = pc
+            for j in range(4):
+                for tt in range(CH):
+                    nc.tensor.matmul(out=pc[:, j:j + 1], lhsT=xn[NCH + c][:, tt, j * P:(j + 1) * P],
+                                     rhs=onesb[:, 0:1], start=(tt == 0), stop=(tt == CH - 1))
+
+        def col_sums_out(c):
+            nc.vector.tensor_copy(out=sums1[:, c, :], in_=pcs[c][:, 0:4])
 
         def mean_of(h):
-            nv = 4 - E1S[h]
+            nv = 4 - E1S[0]
             msum = const.tile([P, 4], F32, name="msum%d" % h)
-            nc.vector.tensor_reduce(out=msum[:, 0:nv], in_=sumsV[h][:], axis=AX.X, op=ALU.add)
-            nc.vector.tensor_reduce(out=msum[:, nv:4], in_=sumsS[h][:], axis=AX.X, op=ALU.add)
+            if h == 0:
+                nc.vector.tensor_reduce(out=msum[:, 0:nv], in_=sumsV[h][:], axis=AX.X, op=ALU.add)
+                nc.vector.tensor_reduce(out=msum[:, nv:4], in_=sumsS[h][:], axis=AX.X, op=ALU.add)
+            else:
+                nc.vector.tensor_reduce(out=msum[:], in_=sums1[:].rearrange("p c j -> p j c"), axis=AX.X,
+                                        op=ALU.add)
             nc.vector.tensor_scalar(out=mean[h][:], in0=msum[:], scalar1=1.0 / N1, scalar2=None, op0=ALU.mult)
             nc.vector.scalar_tensor_tensor(out=nbias[h][:], in0=mean[h][:], scalar=-1.0,
                                            in1=rls[:, 4 * h:4 * h + 4], op0=ALU.mult, op1=ALU.mult)
@@ -190,9 +220,22 @@ def tile_maternkernel_t_kernel(tc, x1, x2, lengthscale, out):
         wt = {}
         et = {}
 
+        ptg = {}
+
+        def t1g(g, b):
+            t = ps1.tile([P, 2, GW], BF16, name="ptg", tag="pt")
+            for pl in range(2):
+                for tl in range(4):
+                    nc.tensor.transpose(t[:, pl, tl * P:(tl + 1) * P],
+                                        xn[NCH + g // 2][:, 4 * (g % 2) + tl, (2 * b + pl) * P:(2 * b + pl + 1) * P],
+                                        identb[:])
+            ptg[(g, b)] = t
+
         def src_of(k, j):
             h, g = k // NG, k % NG
-            return xT[h * NCH + g // 2][:, j, (g % 2) * GW:(g % 2 + 1) * GW]
+            if h == 1:
+                return ptg[(g, j // 2)][:, j % 2, :]
+            return xT[g // 2][:, j, (g % 2) * GW:(g % 2 + 1) * GW]
 
         def st_square(k):
             sq[k] = work.tile([P, 4, GW], F32, name="sq", tag="sq", bufs=2)
@@ -285,16 +328,25 @@ def tile_maternkernel_t_kernel(tc, x1, x2, lengthscale, out):
 
         pending = []
         for s in range(2 * NG + 8):
-            if s < NG:
-                unit(1, 2 * s)
-                unit(1, 2 * s + 1)
+            if NG <= s + 1 < 2 * NG + 1 and s + 1 - NG < NG:
+                t1g(s + 1 - NG, 0)
             if 0 <= s - 1 < 2 * NG:
                 st_quant(s - 1)
                 st_t2(s - 1)
-            if s == NG:
+            for c in range(NCH):
+                when = c + 1 if c < 3 else 2 * c - 2
+                if s == when + 1:
+                    col_sums_out(c)
+                if s == when:
+                    col_sums(c)
+            if s == 14:
                 mean_of(1)
                 bpost(1)
+            if s == 15:
                 sq2_spread()
+            if NG <= s + 1 < 2 * NG + 1 and s + 1 - NG < NG:
+                t1g(s + 1 - NG, 1)
+                idle_passes(IDLE[1])
             todo = pending
             pending = []
             gs = s - NG - 4
@@ -305,8 +357,10 @@ def tile_maternkernel_t_kernel(tc, x1, x2, lengthscale, out):
                         st_exp(g)
                     pending = batch_of[gs]
             if s < 2 * NG:
-                st_square(s)
                 st_affine(s)
+                st_square(s)
+            if s % 2 == 1 and s <= 9:
+                load(NCH + 3 + s // 2)
             if 0 <= s - 2 < 2 * NG:
                 st_red(s - 2)
             if s < 2 * NG:

@@ -10,8 +10,10 @@ E1S = (1, 1)
 BATCH = (5, 5, 4, 2)
 EVERY = 4
 PLAIN = True
+XNB = 3
+XTB = 9
 WARM = 6
-IDLE = (2, 2, 2, 1)
+IDLE = (2, 2, 1, 1)
 
 FP8X4 = mybir.dt.float8_e4m3fn_x4
 BF16 = mybir.dt.bfloat16
@@ -41,7 +43,6 @@ def tile_maternkernel_t_kernel(tc, x1, x2, lengthscale, out):
             ctx.enter_context(tc.manual_schedule())
         const = ctx.enter_context(tc.tile_pool(name="const", bufs=1))
         work = ctx.enter_context(tc.tile_pool(name="work", bufs=2))
-        big = ctx.enter_context(tc.tile_pool(name="big", bufs=1))
         ps1 = ctx.enter_context(tc.psum_pool(name="ps1", bufs=3))
         ps2 = ctx.enter_context(tc.psum_pool(name="ps2", bufs=2))
         psd = ctx.enter_context(tc.psum_pool(name="psd", bufs=1))
@@ -70,17 +71,11 @@ def tile_maternkernel_t_kernel(tc, x1, x2, lengthscale, out):
 
         def load(q):
             h, c = q // NCH, q % NCH
-            if h == 0:
-                slot = 8 + c % 3
-            elif c < 3:
-                slot = 8 + (c + 2) % 3
-            else:
-                slot = c - 3
-            t = big.tile([P, CH, 512], BF16, name="xn", tag="s%d" % slot)
+            t = work.tile([P, CH, 512], BF16, name="xn", tag="xn", bufs=XNB)
             nc.sync.dma_start(out=t[:], in_=x1v[:, c * CH:(c + 1) * CH, h * 512:(h + 1) * 512])
             xn[q] = t
 
-        for q in range(3):
+        for q in range(XNB):
             load(q)
 
         identb = const.tile([P, P], BF16, name="identb")
@@ -113,8 +108,8 @@ def tile_maternkernel_t_kernel(tc, x1, x2, lengthscale, out):
         sqp = [const.tile([P, NT], F32, name="sqp%d" % h) for h in range(2)]
         sq2p = const.tile([P, 2], F32, name="sq2p")
         sq2bc = const.tile([P, P], F32, name="sq2bc")
-        sumsV = [const.tile([P, 4 - E1S[h], NCH], F32, name="sumsV%d" % h) for h in range(1)]
-        sumsS = [const.tile([P, E1S[h], NCH], F32, name="sumsS%d" % h) for h in range(1)]
+        sumsV = [const.tile([P, 4 - E1S[h], NCH], F32, name="sumsV%d" % h) for h in range(2)]
+        sumsS = [const.tile([P, E1S[h], NCH], F32, name="sumsS%d" % h) for h in range(2)]
         mean = [const.tile([P, 4], F32, name="mean%d" % h) for h in range(2)]
         nbias = [const.tile([P, 4], F32, name="nbias%d" % h) for h in range(2)]
 
@@ -124,7 +119,7 @@ def tile_maternkernel_t_kernel(tc, x1, x2, lengthscale, out):
             c, j = u // 4, u % 4
             q = h * NCH + c
             if j == 0:
-                xT[q] = big.tile([P, 4, CH * P], BF16, name="xT", tag="s%d" % c)
+                xT[q] = work.tile([P, 4, CH * P], BF16, name="xT", tag="xT", bufs=XTB)
             pt = ps1.tile([P, 1024], BF16, name="pt", tag="pt")
             for tt in range(CH):
                 nc.tensor.transpose(pt[:, tt * P:(tt + 1) * P], xn[q][:, tt, j * P:(j + 1) * P], identb[:])
@@ -145,34 +140,14 @@ def tile_maternkernel_t_kernel(tc, x1, x2, lengthscale, out):
                         nc.tensor.matmul(out=pd[:, 0:P], lhsT=identf[:], rhs=identf[:], start=True, stop=True)
                 else:
                     idle_passes(IDLE[h])
-            if j == 3 and q + 3 < NCH + 3:
-                load(q + 3)
-
-        onesb = const.tile([P, 2], BF16, name="onesb")
-        nc.vector.memset(onesb[:], 1.0)
-        sums1 = const.tile([P, NCH, 4], F32, name="sums1")
-        pcs = {}
-
-        def col_sums(c):
-            pc = psm.tile([P, 512], F32, name="pc", tag="pm")
-            pcs[c] = pc
-            for j in range(4):
-                for tt in range(CH):
-                    nc.tensor.matmul(out=pc[:, j:j + 1], lhsT=xn[NCH + c][:, tt, j * P:(j + 1) * P],
-                                     rhs=onesb[:, 0:1], start=(tt == 0), stop=(tt == CH - 1))
-
-        def col_sums_out(c):
-            nc.vector.tensor_copy(out=sums1[:, c, :], in_=pcs[c][:, 0:4])
+            if j == 3 and q + XNB < 2 * NCH:
+                load(q + XNB)
 
         def mean_of(h):
-            nv = 4 - E1S[0]
+            nv = 4 - E1S[h]
             msum = const.tile([P, 4], F32, name="msum%d" % h)
-            if h == 0:
-                nc.vector.tensor_reduce(out=msum[:, 0:nv], in_=sumsV[h][:], axis=AX.X, op=ALU.add)
-                nc.vector.tensor_reduce(out=msum[:, nv:4], in_=sumsS[h][:], axis=AX.X, op=ALU.add)
-            else:
-                nc.vector.tensor_reduce(out=msum[:], in_=sums1[:].rearrange("p c j -> p j c"), axis=AX.X,
-                                        op=ALU.add)
+            nc.vector.tensor_reduce(out=msum[:, 0:nv], in_=sumsV[h][:], axis=AX.X, op=ALU.add)
+            nc.vector.tensor_reduce(out=msum[:, nv:4], in_=sumsS[h][:], axis=AX.X, op=ALU.add)
             nc.vector.tensor_scalar(out=mean[h][:], in0=msum[:], scalar1=1.0 / N1, scalar2=None, op0=ALU.mult)
             nc.vector.scalar_tensor_tensor(out=nbias[h][:], in0=mean[h][:], scalar=-1.0,
                                            in1=rls[:, 4 * h:4 * h + 4], op0=ALU.mult, op1=ALU.mult)
@@ -220,25 +195,12 @@ def tile_maternkernel_t_kernel(tc, x1, x2, lengthscale, out):
         wt = {}
         et = {}
 
-        ptg = {}
-
-        def t1g(g, b):
-            t = ps1.tile([P, 2, GW], BF16, name="ptg", tag="pt")
-            for pl in range(2):
-                for tl in range(4):
-                    nc.tensor.transpose(t[:, pl, tl * P:(tl + 1) * P],
-                                        xn[NCH + g // 2][:, 4 * (g % 2) + tl, (2 * b + pl) * P:(2 * b + pl + 1) * P],
-                                        identb[:])
-            ptg[(g, b)] = t
-
         def src_of(k, j):
             h, g = k // NG, k % NG
-            if h == 1:
-                return ptg[(g, j // 2)][:, j % 2, :]
-            return xT[g // 2][:, j, (g % 2) * GW:(g % 2 + 1) * GW]
+            return xT[h * NCH + g // 2][:, j, (g % 2) * GW:(g % 2 + 1) * GW]
 
         def st_square(k):
-            sq[k] = work.tile([P, 4, GW], F32, name="sq", tag="sq", bufs=2)
+            sq[k] = work.tile([P, 4, GW], F32, name="sq", tag="sq", bufs=3)
             for j in range(4):
                 square(k // NG, j, sq[k][:, j, :], src_of(k, j))
 
@@ -328,25 +290,16 @@ def tile_maternkernel_t_kernel(tc, x1, x2, lengthscale, out):
 
         pending = []
         for s in range(2 * NG + 8):
-            if NG <= s + 1 < 2 * NG + 1 and s + 1 - NG < NG:
-                t1g(s + 1 - NG, 0)
+            if s < NG:
+                unit(1, 2 * s)
+                unit(1, 2 * s + 1)
             if 0 <= s - 1 < 2 * NG:
                 st_quant(s - 1)
                 st_t2(s - 1)
-            for c in range(NCH):
-                when = c + 1 if c < 3 else 2 * c - 2
-                if s == when + 1:
-                    col_sums_out(c)
-                if s == when:
-                    col_sums(c)
-            if s == 14:
+            if s == NG:
                 mean_of(1)
                 bpost(1)
-            if s == 15:
                 sq2_spread()
-            if NG <= s + 1 < 2 * NG + 1 and s + 1 - NG < NG:
-                t1g(s + 1 - NG, 1)
-                idle_passes(IDLE[1])
             todo = pending
             pending = []
             gs = s - NG - 4
@@ -357,10 +310,8 @@ def tile_maternkernel_t_kernel(tc, x1, x2, lengthscale, out):
                         st_exp(g)
                     pending = batch_of[gs]
             if s < 2 * NG:
-                st_affine(s)
                 st_square(s)
-            if s % 2 == 1 and s <= 9:
-                load(NCH + 3 + s // 2)
+                st_affine(s)
             if 0 <= s - 2 < 2 * NG:
                 st_red(s - 2)
             if s < 2 * NG:

@@ -5,15 +5,15 @@ from concourse.masks import make_identity
 
 FLOPS = 2 * 8192 * 128 * 1024
 
-MANUAL = False
-E1S = (1, 1)
 BATCH = (5, 5, 4, 2)
-EVERY = 4
-PLAIN = True
-XNB = 3
-XTB = 9
+E1S = 1
+VJ = ()
+XNB = 6
+XTB = 8
+LAG = 1
+MEAN1 = 4
 WARM = 6
-IDLE = (2, 2, 1, 1)
+IDLE = 1
 
 FP8X4 = mybir.dt.float8_e4m3fn_x4
 BF16 = mybir.dt.bfloat16
@@ -30,6 +30,7 @@ D = 1024
 NT = N1 // P
 CH = 8
 NCH = NT // CH
+CW = CH * P
 GW = 512
 NG = N1 // GW
 
@@ -39,44 +40,29 @@ def tile_maternkernel_t_kernel(tc, x1, x2, lengthscale, out):
     x1v = x1.rearrange("(p t) f -> p t f", t=NT)
     outv = out.rearrange("(p t) n -> p t n", t=NT)
     with ExitStack() as ctx:
-        if MANUAL:
-            ctx.enter_context(tc.manual_schedule())
         const = ctx.enter_context(tc.tile_pool(name="const", bufs=1))
         work = ctx.enter_context(tc.tile_pool(name="work", bufs=2))
-        ps1 = ctx.enter_context(tc.psum_pool(name="ps1", bufs=3))
+        ps1 = ctx.enter_context(tc.psum_pool(name="ps1", bufs=4))
         ps2 = ctx.enter_context(tc.psum_pool(name="ps2", bufs=2))
         psd = ctx.enter_context(tc.psum_pool(name="psd", bufs=1))
-        psm = ctx.enter_context(tc.psum_pool(name="psm", bufs=2))
+        psm = ctx.enter_context(tc.psum_pool(name="psm", bufs=1))
 
-        zb = const.tile([P, 2048], BF16, name="zb", align_bytes=64)
-        nc.vector.memset(zb[:], 1.0)
-        zc = const.tile([P, 512], U32, name="zc", align_bytes=64)
-        zs = const.tile([P, 512], U8, name="zs", align_bytes=64)
-        nc.vector.quantize_mx(out=zc[:].bitcast(FP8X4), scales=zs[:], in_=zb[:])
-        pd = psd.tile([P, 512], F32, name="pd")
-
-        def idle_passes(n):
-            for i in range(n):
-                nc.tensor.matmul_mx(out=pd[:], lhsT=zc[:, 0:P].bitcast(FP8X4), lhsT_scale=zs[:, 0:P],
-                                    rhs=zc[:].bitcast(FP8X4), rhs_scale=zs[:], start=True, stop=True)
-
-        idle_passes(WARM)
         lsz = const.tile([P, P], BF16, name="lsz")
         nc.vector.memset(lsz[:], 0.0)
         nc.scalar.dma_start(out=lsz[0:8, :], in_=lengthscale.rearrange("(k p) -> k p", p=P))
         x2n = const.tile([P, D], BF16, name="x2n")
         nc.scalar.dma_start(out=x2n[:], in_=x2)
+        zb = const.tile([P, 1024], BF16, name="zb", align_bytes=64)
+        nc.vector.memset(zb[:], 1.0)
+        zc = const.tile([P, 256], U32, name="zc", align_bytes=64)
+        zs = const.tile([P, 256], U8, name="zs", align_bytes=64)
+        nc.vector.quantize_mx(out=zc[:].bitcast(FP8X4), scales=zs[:], in_=zb[:])
+        pd = psd.tile([P, 512], F32, name="pd")
+        PM1 = 256
 
-        xn = {}
-
-        def load(q):
-            h, c = q // NCH, q % NCH
-            t = work.tile([P, CH, 512], BF16, name="xn", tag="xn", bufs=XNB)
-            nc.sync.dma_start(out=t[:], in_=x1v[:, c * CH:(c + 1) * CH, h * 512:(h + 1) * 512])
-            xn[q] = t
-
-        for q in range(XNB):
-            load(q)
+        for i in range(WARM):
+            nc.tensor.matmul_mx(out=pd[:, 0:256], lhsT=zc[:, 0:P].bitcast(FP8X4), lhsT_scale=zs[:, 0:P],
+                                rhs=zc[:].bitcast(FP8X4), rhs_scale=zs[:], start=True, stop=True)
 
         identb = const.tile([P, P], BF16, name="identb")
         make_identity(nc, identb[:])
@@ -84,22 +70,14 @@ def tile_maternkernel_t_kernel(tc, x1, x2, lengthscale, out):
         make_identity(nc, identf[:])
         ones = const.tile([P, P], F32, name="ones")
         nc.vector.memset(ones[:], 1.0)
+        oneb = const.tile([P, 1], BF16, name="oneb")
+        nc.vector.memset(oneb[:], 1.0)
         warm = const.tile([P, 1], F32, name="warm")
         nc.scalar.activation(out=warm[:], in_=ones[:, 0:1], func=ACT.Sqrt)
 
         lsT = const.tile([P, 8], F32, name="lsT")
         rls = const.tile([P, 8], F32, name="rls")
         x2T = const.tile([P, 8, P], BF16, name="x2T")
-
-        def small_inputs():
-            pl = ps1.tile([P, 1024], BF16, name="pl", tag="pt")
-            nc.tensor.transpose(pl[:, 0:P], lsz[:], identb[:])
-            nc.vector.tensor_copy(out=lsT[:], in_=pl[:, 0:8])
-            nc.vector.reciprocal(out=rls[:], in_=lsT[:])
-            px = ps1.tile([P, 1024], BF16, name="px", tag="pt")
-            for kt in range(8):
-                nc.tensor.transpose(px[:, kt * P:(kt + 1) * P], x2n[:, kt * P:(kt + 1) * P], identb[:])
-            nc.vector.tensor_copy(out=x2T[:].rearrange("p k n -> p (k n)"), in_=px[:])
 
         codes0 = const.tile([P, N1], U32, name="codes0", align_bytes=64)
         scales0 = const.tile([P, N1], U8, name="scales0", align_bytes=64)
@@ -108,46 +86,68 @@ def tile_maternkernel_t_kernel(tc, x1, x2, lengthscale, out):
         sqp = [const.tile([P, NT], F32, name="sqp%d" % h) for h in range(2)]
         sq2p = const.tile([P, 2], F32, name="sq2p")
         sq2bc = const.tile([P, P], F32, name="sq2bc")
-        sumsV = [const.tile([P, 4 - E1S[h], NCH], F32, name="sumsV%d" % h) for h in range(2)]
-        sumsS = [const.tile([P, E1S[h], NCH], F32, name="sumsS%d" % h) for h in range(2)]
+        sumsV = const.tile([P, 4 - E1S, NCH], F32, name="sumsV")
+        sumsS = const.tile([P, E1S, NCH], F32, name="sumsS")
         mean = [const.tile([P, 4], F32, name="mean%d" % h) for h in range(2)]
         nbias = [const.tile([P, 4], F32, name="nbias%d" % h) for h in range(2)]
 
         xT = {}
+        xn = {}
 
-        def unit(h, u):
-            c, j = u // 4, u % 4
+        def load(q):
+            h, c = q // NCH, q % NCH
+            xn[q] = work.tile([P, CH, 512], BF16, name="xn", tag="xn", bufs=XNB)
+            nc.sync.dma_start(out=xn[q][:], in_=x1v[:, c * CH:(c + 1) * CH, h * 512:(h + 1) * 512])
+
+        def transposes(h, c, j):
             q = h * NCH + c
-            if j == 0:
-                xT[q] = work.tile([P, 4, CH * P], BF16, name="xT", tag="xT", bufs=XTB)
-            pt = ps1.tile([P, 1024], BF16, name="pt", tag="pt")
+            pt = ps1.tile([P, CW], BF16, name="pt", tag="pt")
             for tt in range(CH):
-                nc.tensor.transpose(pt[:, tt * P:(tt + 1) * P], xn[q][:, tt, j * P:(j + 1) * P], identb[:])
-            nv = 4 - E1S[h]
-            if j < nv:
-                nc.vector.tensor_scalar(out=xT[q][:, j, :], in0=pt[:], scalar1=1.0, scalar2=None,
-                                        op0=ALU.mult, op1=ALU.add, accum_out=sumsV[h][:, j, c:c + 1])
-            else:
-                nc.scalar.activation(out=xT[q][:, j, :], in_=pt[:], func=ACT.Copy,
-                                     accum_out=sumsS[h][:, j - nv, c:c + 1])
-            if h == 0 and PLAIN and EVERY == 4:
-                if j == 3:
-                    for i in range(IDLE[h]):
-                        nc.tensor.matmul(out=pd[:, 0:P], lhsT=identf[:], rhs=identf[:], start=True, stop=True)
-            elif j % 2 == 1:
-                if h == 0 and PLAIN:
-                    for i in range(IDLE[h]):
-                        nc.tensor.matmul(out=pd[:, 0:P], lhsT=identf[:], rhs=identf[:], start=True, stop=True)
+                src = xn[q][:, tt, j * P:(j + 1) * P]
+                if h == 0 and (tt == 7 or (tt == 3 and j % 2 == 1)):
+                    nc.tensor.matmul(out=pt[:, tt * P:(tt + 1) * P], lhsT=src, rhs=identb[:], start=True, stop=True)
                 else:
-                    idle_passes(IDLE[h])
-            if j == 3 and q + XNB < 2 * NCH:
-                load(q + XNB)
+                    nc.tensor.transpose(pt[:, tt * P:(tt + 1) * P], src, identb[:])
+            return pt
+
+        def unit0(c, j):
+            if j == 0:
+                xT[c] = work.tile([P, 4, CW], BF16, name="xT", tag="xT", bufs=XTB)
+            pt = transposes(0, c, j)
+            nv = 4 - E1S
+            if j < nv:
+                nc.vector.tensor_scalar(out=xT[c][:, j, :], in0=pt[:], scalar1=1.0, scalar2=None,
+                                        op0=ALU.mult, op1=ALU.add, accum_out=sumsV[:, j, c:c + 1])
+            else:
+                nc.scalar.activation(out=xT[c][:, j, :], in_=pt[:], func=ACT.Copy,
+                                     accum_out=sumsS[:, j - nv, c:c + 1])
+
+        def unit1(c, j):
+            q = NCH + c
+            if j == 0:
+                xT[q] = work.tile([P, 4, CW], BF16, name="xT", tag="xT", bufs=XTB)
+            pt = transposes(1, c, j)
+            if j in VJ:
+                nc.vector.tensor_copy(out=xT[q][:, j, :], in_=pt[:])
+            else:
+                nc.scalar.copy(out=xT[q][:, j, :], in_=pt[:])
+
+        def row_sums1(c):
+            for j in range(4):
+                for tt in range(CH):
+                    nc.tensor.matmul(out=pd[:, PM1 + 8 * j + c:PM1 + 8 * j + c + 1],
+                                     lhsT=xn[NCH + c][:, tt, j * P:(j + 1) * P], rhs=oneb[:],
+                                     start=(tt == 0), stop=(tt == CH - 1))
 
         def mean_of(h):
-            nv = 4 - E1S[h]
             msum = const.tile([P, 4], F32, name="msum%d" % h)
-            nc.vector.tensor_reduce(out=msum[:, 0:nv], in_=sumsV[h][:], axis=AX.X, op=ALU.add)
-            nc.vector.tensor_reduce(out=msum[:, nv:4], in_=sumsS[h][:], axis=AX.X, op=ALU.add)
+            if h == 0:
+                nv = 4 - E1S
+                nc.vector.tensor_reduce(out=msum[:, 0:nv], in_=sumsV[:], axis=AX.X, op=ALU.add)
+                nc.vector.tensor_reduce(out=msum[:, nv:4], in_=sumsS[:], axis=AX.X, op=ALU.add)
+            else:
+                nc.vector.tensor_reduce(out=msum[:], in_=pd[:, PM1:PM1 + 32].rearrange("p (j c) -> p j c", c=NCH),
+                                        axis=AX.X, op=ALU.add)
             nc.vector.tensor_scalar(out=mean[h][:], in0=msum[:], scalar1=1.0 / N1, scalar2=None, op0=ALU.mult)
             nc.vector.scalar_tensor_tensor(out=nbias[h][:], in0=mean[h][:], scalar=-1.0,
                                            in1=rls[:, 4 * h:4 * h + 4], op0=ALU.mult, op1=ALU.mult)
@@ -161,12 +161,12 @@ def tile_maternkernel_t_kernel(tc, x1, x2, lengthscale, out):
                                  scale=rls[:, 4 * h + j:4 * h + j + 1])
 
         def bpost(h):
-            abb = const.tile([P, 4, P], BF16, name="abb%d" % h)
-            sqb = const.tile([P, 4, P], F32, name="sqb%d" % h)
+            abb = const.tile([P, 4, P], BF16, name="abb", tag="abb", bufs=1)
+            sqb = const.tile([P, 4, P], F32, name="sqb", tag="sqb", bufs=1)
             for j in range(4):
                 square(h, j, sqb[:, j, :], x2T[:, 4 * h + j, :])
                 affine(h, j, abb[:, j, :], x2T[:, 4 * h + j, :])
-            grb = const.tile([P, P, 4], BF16, name="grb%d" % h, align_bytes=64)
+            grb = const.tile([P, P, 4], BF16, name="grb", tag="grb", bufs=1, align_bytes=64)
             nc.vector.tensor_copy(out=grb[:], in_=abb[:].rearrange("p j r -> p r j"))
             nc.vector.quantize_mx(out=bcodes[h][:].bitcast(FP8X4), scales=bscales[h][:],
                                   in_=grb[:].rearrange("p r j -> p (r j)"))
@@ -220,8 +220,8 @@ def tile_maternkernel_t_kernel(tc, x1, x2, lengthscale, out):
                 cod[k] = codes0[:, g * GW:(g + 1) * GW]
                 sca[k] = scales0[:, g * GW:(g + 1) * GW]
             else:
-                c1 = work.tile([P, GW], U32, name="c1", tag="c1", bufs=4, align_bytes=64)
-                s1 = work.tile([P, GW], U8, name="s1", tag="s1", bufs=4, align_bytes=64)
+                c1 = work.tile([P, GW], U32, name="c1", tag="c1", bufs=2, align_bytes=64)
+                s1 = work.tile([P, GW], U8, name="s1", tag="s1", bufs=2, align_bytes=64)
                 cod[k] = c1[:]
                 sca[k] = s1[:]
             nc.vector.quantize_mx(out=cod[k].bitcast(FP8X4), scales=sca[k],
@@ -233,7 +233,11 @@ def tile_maternkernel_t_kernel(tc, x1, x2, lengthscale, out):
                 for j in range(4):
                     nc.tensor.matmul(out=pa[k][:, tl * P:(tl + 1) * P], lhsT=sq[k][:, j, tl * P:(tl + 1) * P],
                                      rhs=identf[:], is_transpose=True, start=(j == 0), stop=(j == 3))
-            idle_passes(IDLE[2 + k // NG])
+            h = k // NG
+            for i in range(IDLE):
+                nc.tensor.matmul_mx(out=pd[:, 0:256], lhsT=bcodes[h][:].bitcast(FP8X4), lhsT_scale=bscales[h][:],
+                                    rhs=cod[k][:, 0:256].bitcast(FP8X4), rhs_scale=sca[k][:, 0:256],
+                                    start=True, stop=True)
 
         def st_red(k):
             h, g = k // NG, k % NG
@@ -255,7 +259,7 @@ def tile_maternkernel_t_kernel(tc, x1, x2, lengthscale, out):
             sq1g = work.tile([P, 4], F32, name="sq1g", tag="sq1g", bufs=3)
             nc.vector.tensor_tensor(out=sq1g[:], in0=sqp[0][:, 4 * g:4 * g + 4], in1=sqp[1][:, 4 * g:4 * g + 4],
                                     op=ALU.add)
-            wt[g] = work.tile([P, 4, P], F32, name="wt", tag="wt", bufs=8)
+            wt[g] = work.tile([P, 4, P], F32, name="wt", tag="wt", bufs=6)
             nc.vector.scalar_tensor_tensor(out=wt[g][:], in0=pm[g][:].rearrange("p (t n) -> p t n", n=P),
                                            scalar=-2.0, in1=sq2bc[:].unsqueeze(1).to_broadcast([P, 4, P]),
                                            op0=ALU.mult, op1=ALU.add)
@@ -267,7 +271,7 @@ def tile_maternkernel_t_kernel(tc, x1, x2, lengthscale, out):
             nc.scalar.activation(out=wt[g][:], in_=wt[g][:], func=ACT.Sqrt, scale=3.0)
 
         def st_exp(g):
-            et[g] = work.tile([P, 4, P], F32, name="et", tag="et", bufs=5)
+            et[g] = work.tile([P, 4, P], F32, name="et", tag="et", bufs=3)
             nc.scalar.activation(out=et[g][:], in_=wt[g][:], func=ACT.Exp, scale=-1.0)
 
         def st_out(g):
@@ -281,25 +285,43 @@ def tile_maternkernel_t_kernel(tc, x1, x2, lengthscale, out):
             batch_of[g0 + b - 1] = list(range(g0, g0 + b))
             g0 += b
 
-        for u in range(4 * NCH):
-            unit(0, u)
-            if u == 11:
-                small_inputs()
+        for q in range(XNB):
+            load(q)
+        for c in range(NCH):
+            for j in range(4):
+                unit0(c, j)
+            load(c + XNB)
+            if c == 2:
+                pl = ps1.tile([P, CW], BF16, name="pl", tag="pt")
+                nc.tensor.transpose(pl[:, 0:P], lsz[:], identb[:])
+                nc.vector.tensor_copy(out=lsT[:], in_=pl[:, 0:8])
+                nc.vector.reciprocal(out=rls[:], in_=lsT[:])
+                px = ps1.tile([P, CW], BF16, name="px", tag="pt")
+                for kt in range(8):
+                    nc.tensor.transpose(px[:, kt * P:(kt + 1) * P], x2n[:, kt * P:(kt + 1) * P], identb[:])
+                nc.vector.tensor_copy(out=x2T[:].rearrange("p k n -> p (k n)"), in_=px[:])
         mean_of(0)
         bpost(0)
 
         pending = []
         for s in range(2 * NG + 8):
-            if s < NG:
-                unit(1, 2 * s)
-                unit(1, 2 * s + 1)
-            if 0 <= s - 1 < 2 * NG:
-                st_quant(s - 1)
-                st_t2(s - 1)
-            if s == NG:
+            c2 = s // 2 - LAG
+            if 0 <= c2 < NCH:
+                unit1(c2, 2 * (s % 2))
+                unit1(c2, 2 * (s % 2) + 1)
+                if s % 2 == 1 and NCH + c2 + XNB < 2 * NCH:
+                    load(NCH + c2 + XNB)
+            if s < XNB:
+                row_sums1(s)
+            if XNB <= s // 2 - LAG + XNB - 1 < NCH and s % 2 == 1:
+                row_sums1(s // 2 - LAG + XNB - 1)
+            if s == 2 * MEAN1:
                 mean_of(1)
                 bpost(1)
                 sq2_spread()
+            if 0 <= s - 1 < 2 * NG:
+                st_quant(s - 1)
+                st_t2(s - 1)
             todo = pending
             pending = []
             gs = s - NG - 4

@@ -12,8 +12,9 @@ XNB = 6
 XTB = 8
 LAG = 1
 MEAN1 = 4
-WARM = 6
-IDLE = 1
+WARM = 10
+IDLE = (1, 2)
+IDLET = 1
 
 FP8X4 = mybir.dt.float8_e4m3fn_x4
 BF16 = mybir.dt.bfloat16
@@ -42,7 +43,7 @@ def tile_maternkernel_t_kernel(tc, x1, x2, lengthscale, out):
     with ExitStack() as ctx:
         const = ctx.enter_context(tc.tile_pool(name="const", bufs=1))
         work = ctx.enter_context(tc.tile_pool(name="work", bufs=2))
-        ps1 = ctx.enter_context(tc.psum_pool(name="ps1", bufs=4))
+        ps1 = ctx.enter_context(tc.psum_pool(name="ps1", bufs=3))
         ps2 = ctx.enter_context(tc.psum_pool(name="ps2", bufs=2))
         psd = ctx.enter_context(tc.psum_pool(name="psd", bufs=1))
         psm = ctx.enter_context(tc.psum_pool(name="psm", bufs=1))
@@ -57,7 +58,8 @@ def tile_maternkernel_t_kernel(tc, x1, x2, lengthscale, out):
         zc = const.tile([P, 256], U32, name="zc", align_bytes=64)
         zs = const.tile([P, 256], U8, name="zs", align_bytes=64)
         nc.vector.quantize_mx(out=zc[:].bitcast(FP8X4), scales=zs[:], in_=zb[:])
-        pd = psd.tile([P, 512], F32, name="pd")
+        pd = psd.tile([P, 512], F32, name="pd", tag="pd")
+        pi = psd.tile([P, 512], F32, name="pi", tag="pi")
         PM1 = 256
 
         for i in range(WARM):
@@ -227,17 +229,19 @@ def tile_maternkernel_t_kernel(tc, x1, x2, lengthscale, out):
             nc.vector.quantize_mx(out=cod[k].bitcast(FP8X4), scales=sca[k],
                                   in_=gr[k][:].rearrange("p r j -> p (r j)"))
 
+        def idle(k, n):
+            h = k // NG
+            for i in range(n):
+                nc.tensor.matmul_mx(out=pi[:], lhsT=bcodes[h][:].bitcast(FP8X4), lhsT_scale=bscales[h][:],
+                                    rhs=cod[k].bitcast(FP8X4), rhs_scale=sca[k], start=True, stop=True)
+
         def st_t2(k):
             pa[k] = ps2.tile([P, 512], F32, name="pa", tag="pa")
             for tl in range(4):
                 for j in range(4):
                     nc.tensor.matmul(out=pa[k][:, tl * P:(tl + 1) * P], lhsT=sq[k][:, j, tl * P:(tl + 1) * P],
                                      rhs=identf[:], is_transpose=True, start=(j == 0), stop=(j == 3))
-            h = k // NG
-            for i in range(IDLE):
-                nc.tensor.matmul_mx(out=pd[:, 0:256], lhsT=bcodes[h][:].bitcast(FP8X4), lhsT_scale=bscales[h][:],
-                                    rhs=cod[k][:, 0:256].bitcast(FP8X4), rhs_scale=sca[k][:, 0:256],
-                                    start=True, stop=True)
+            idle(k, IDLE[k // NG])
 
         def st_red(k):
             h, g = k // NG, k % NG
@@ -309,6 +313,7 @@ def tile_maternkernel_t_kernel(tc, x1, x2, lengthscale, out):
             if 0 <= c2 < NCH:
                 unit1(c2, 2 * (s % 2))
                 unit1(c2, 2 * (s % 2) + 1)
+                idle(max(0, s - 2), IDLET)
                 if s % 2 == 1 and NCH + c2 + XNB < 2 * NCH:
                     load(NCH + c2 + XNB)
             if s < XNB:

@@ -12,8 +12,10 @@ XNB = 6
 XTB = 8
 LAG = 1
 MEAN1 = 4
-WARM = 10
+WARM = 5
 IDLE = (1, 2)
+IDLEH = 2
+RN = 16
 IDLET = 1
 
 FP8X4 = mybir.dt.float8_e4m3fn_x4
@@ -55,16 +57,18 @@ def tile_maternkernel_t_kernel(tc, x1, x2, lengthscale, out):
         nc.scalar.dma_start(out=x2n[:], in_=x2)
         zb = const.tile([P, 1024], BF16, name="zb", align_bytes=64)
         nc.vector.memset(zb[:], 1.0)
-        zc = const.tile([P, 256], U32, name="zc", align_bytes=64)
-        zs = const.tile([P, 256], U8, name="zs", align_bytes=64)
-        nc.vector.quantize_mx(out=zc[:].bitcast(FP8X4), scales=zs[:], in_=zb[:])
-        pd = psd.tile([P, 512], F32, name="pd", tag="pd")
+        zc = const.tile([P, 512], U32, name="zc", align_bytes=64)
+        zs = const.tile([P, 512], U8, name="zs", align_bytes=64)
+        for i in range(2):
+            nc.vector.quantize_mx(out=zc[:, 256 * i:256 * i + 256].bitcast(FP8X4),
+                                  scales=zs[:, 256 * i:256 * i + 256], in_=zb[:])
+        pd = psd.tile([P, 4, NCH, RN], F32, name="pd", tag="pd")
         pi = psd.tile([P, 512], F32, name="pi", tag="pi")
-        PM1 = 256
 
-        for i in range(WARM):
-            nc.tensor.matmul_mx(out=pd[:, 0:256], lhsT=zc[:, 0:P].bitcast(FP8X4), lhsT_scale=zs[:, 0:P],
-                                rhs=zc[:].bitcast(FP8X4), rhs_scale=zs[:], start=True, stop=True)
+        def idle0(n):
+            for i in range(n):
+                nc.tensor.matmul_mx(out=pi[:], lhsT=zc[:, 0:P].bitcast(FP8X4), lhsT_scale=zs[:, 0:P],
+                                    rhs=zc[:].bitcast(FP8X4), rhs_scale=zs[:], start=True, stop=True)
 
         identb = const.tile([P, P], BF16, name="identb")
         make_identity(nc, identb[:])
@@ -72,7 +76,7 @@ def tile_maternkernel_t_kernel(tc, x1, x2, lengthscale, out):
         make_identity(nc, identf[:])
         ones = const.tile([P, P], F32, name="ones")
         nc.vector.memset(ones[:], 1.0)
-        oneb = const.tile([P, 1], BF16, name="oneb")
+        oneb = const.tile([P, RN], BF16, name="oneb")
         nc.vector.memset(oneb[:], 1.0)
         warm = const.tile([P, 1], F32, name="warm")
         nc.scalar.activation(out=warm[:], in_=ones[:, 0:1], func=ACT.Sqrt)
@@ -106,7 +110,7 @@ def tile_maternkernel_t_kernel(tc, x1, x2, lengthscale, out):
             pt = ps1.tile([P, CW], BF16, name="pt", tag="pt")
             for tt in range(CH):
                 src = xn[q][:, tt, j * P:(j + 1) * P]
-                if h == 0 and (tt == 7 or (tt == 3 and j % 2 == 1)):
+                if h == 0 and tt == 7 and j % 2 == 1:
                     nc.tensor.matmul(out=pt[:, tt * P:(tt + 1) * P], lhsT=src, rhs=identb[:], start=True, stop=True)
                 else:
                     nc.tensor.transpose(pt[:, tt * P:(tt + 1) * P], src, identb[:])
@@ -137,8 +141,7 @@ def tile_maternkernel_t_kernel(tc, x1, x2, lengthscale, out):
         def row_sums1(c):
             for j in range(4):
                 for tt in range(CH):
-                    nc.tensor.matmul(out=pd[:, PM1 + 8 * j + c:PM1 + 8 * j + c + 1],
-                                     lhsT=xn[NCH + c][:, tt, j * P:(j + 1) * P], rhs=oneb[:],
+                    nc.tensor.matmul(out=pd[:, j, c, :], lhsT=xn[NCH + c][:, tt, j * P:(j + 1) * P], rhs=oneb[:],
                                      start=(tt == 0), stop=(tt == CH - 1))
 
         def mean_of(h):
@@ -148,7 +151,7 @@ def tile_maternkernel_t_kernel(tc, x1, x2, lengthscale, out):
                 nc.vector.tensor_reduce(out=msum[:, 0:nv], in_=sumsV[:], axis=AX.X, op=ALU.add)
                 nc.vector.tensor_reduce(out=msum[:, nv:4], in_=sumsS[:], axis=AX.X, op=ALU.add)
             else:
-                nc.vector.tensor_reduce(out=msum[:], in_=pd[:, PM1:PM1 + 32].rearrange("p (j c) -> p j c", c=NCH),
+                nc.vector.tensor_reduce(out=msum[:], in_=pd[:, :, :, 0],
                                         axis=AX.X, op=ALU.add)
             nc.vector.tensor_scalar(out=mean[h][:], in0=msum[:], scalar1=1.0 / N1, scalar2=None, op0=ALU.mult)
             nc.vector.scalar_tensor_tensor(out=nbias[h][:], in0=mean[h][:], scalar=-1.0,
@@ -291,19 +294,23 @@ def tile_maternkernel_t_kernel(tc, x1, x2, lengthscale, out):
 
         for q in range(XNB):
             load(q)
-        for c in range(NCH):
-            for j in range(4):
-                unit0(c, j)
-            load(c + XNB)
-            if c == 2:
-                pl = ps1.tile([P, CW], BF16, name="pl", tag="pt")
-                nc.tensor.transpose(pl[:, 0:P], lsz[:], identb[:])
-                nc.vector.tensor_copy(out=lsT[:], in_=pl[:, 0:8])
-                nc.vector.reciprocal(out=rls[:], in_=lsT[:])
-                px = ps1.tile([P, CW], BF16, name="px", tag="pt")
-                for kt in range(8):
-                    nc.tensor.transpose(px[:, kt * P:(kt + 1) * P], x2n[:, kt * P:(kt + 1) * P], identb[:])
-                nc.vector.tensor_copy(out=x2T[:].rearrange("p k n -> p (k n)"), in_=px[:])
+        with tc.manual_schedule(engines={mybir.EngineType.PE}):
+            idle0(WARM)
+            for c in range(NCH):
+                if c > 0:
+                    idle0(IDLEH)
+                for j in range(4):
+                    unit0(c, j)
+                load(c + XNB)
+                if c == 2:
+                    pl = ps1.tile([P, CW], BF16, name="pl", tag="pt")
+                    nc.tensor.transpose(pl[:, 0:P], lsz[:], identb[:])
+                    nc.vector.tensor_copy(out=lsT[:], in_=pl[:, 0:8])
+                    nc.vector.reciprocal(out=rls[:], in_=lsT[:])
+                    px = ps1.tile([P, CW], BF16, name="px", tag="pt")
+                    for kt in range(8):
+                        nc.tensor.transpose(px[:, kt * P:(kt + 1) * P], x2n[:, kt * P:(kt + 1) * P], identb[:])
+                    nc.vector.tensor_copy(out=x2T[:].rearrange("p k n -> p (k n)"), in_=px[:])
         mean_of(0)
         bpost(0)
 

@@ -12,11 +12,11 @@ XNB = 6
 XTB = 8
 LAG = 1
 MEAN1 = 4
-WARM = 5
-IDLE = (1, 2)
-IDLEH = 2
+WARM = 14
+IDLE = (2, 2)
+BURST = 6
 RN = 16
-IDLET = 1
+IDLET = 2
 
 FP8X4 = mybir.dt.float8_e4m3fn_x4
 BF16 = mybir.dt.bfloat16
@@ -294,25 +294,25 @@ def tile_maternkernel_t_kernel(tc, x1, x2, lengthscale, out):
 
         for q in range(XNB):
             load(q)
-        with tc.manual_schedule(engines={mybir.EngineType.PE}):
-            idle0(WARM)
-            for c in range(NCH):
-                if c > 0:
-                    idle0(IDLEH)
-                for j in range(4):
-                    unit0(c, j)
-                load(c + XNB)
-                if c == 2:
-                    pl = ps1.tile([P, CW], BF16, name="pl", tag="pt")
-                    nc.tensor.transpose(pl[:, 0:P], lsz[:], identb[:])
-                    nc.vector.tensor_copy(out=lsT[:], in_=pl[:, 0:8])
-                    nc.vector.reciprocal(out=rls[:], in_=lsT[:])
-                    px = ps1.tile([P, CW], BF16, name="px", tag="pt")
-                    for kt in range(8):
-                        nc.tensor.transpose(px[:, kt * P:(kt + 1) * P], x2n[:, kt * P:(kt + 1) * P], identb[:])
-                    nc.vector.tensor_copy(out=x2T[:].rearrange("p k n -> p (k n)"), in_=px[:])
+        idle0(WARM)
+        for c in range(NCH):
+            for j in range(4):
+                unit0(c, j)
+            load(c + XNB)
+            if c == 2:
+                pl = ps1.tile([P, CW], BF16, name="pl", tag="pt")
+                nc.tensor.transpose(pl[:, 0:P], lsz[:], identb[:])
+                nc.vector.tensor_copy(out=lsT[:], in_=pl[:, 0:8])
+                nc.vector.reciprocal(out=rls[:], in_=lsT[:])
+                px = ps1.tile([P, CW], BF16, name="px", tag="pt")
+                for kt in range(8):
+                    nc.tensor.transpose(px[:, kt * P:(kt + 1) * P], x2n[:, kt * P:(kt + 1) * P], identb[:])
+                nc.vector.tensor_copy(out=x2T[:].rearrange("p k n -> p (k n)"), in_=px[:])
         mean_of(0)
         bpost(0)
+        for i in range(BURST):
+            nc.tensor.matmul_mx(out=pi[:], lhsT=bcodes[0][:].bitcast(FP8X4), lhsT_scale=bscales[0][:],
+                                rhs=zc[:].bitcast(FP8X4), rhs_scale=zs[:], start=True, stop=True)
 
         pending = []
         for s in range(2 * NG + 8):

@@ -5,18 +5,17 @@ from concourse.masks import make_identity
 
 FLOPS = 2 * 8192 * 128 * 1024
 
-BATCH = (5, 5, 4, 2)
+BATCH = (7, 6, 3)
 E1S = 1
-VJ = ()
-XNB = 6
+SJ = ()
+XNB = 8
 XTB = 8
-LAG = 1
-MEAN1 = 4
-WARM = 14
-IDLE = (2, 2)
-BURST = 6
-RN = 16
+AHEAD = 2
+WARM = 6
+BURST = 4
+IDLE = (3, 1)
 IDLET = 2
+RN = 16
 
 FP8X4 = mybir.dt.float8_e4m3fn_x4
 BF16 = mybir.dt.bfloat16
@@ -45,7 +44,7 @@ def tile_maternkernel_t_kernel(tc, x1, x2, lengthscale, out):
     with ExitStack() as ctx:
         const = ctx.enter_context(tc.tile_pool(name="const", bufs=1))
         work = ctx.enter_context(tc.tile_pool(name="work", bufs=2))
-        ps1 = ctx.enter_context(tc.psum_pool(name="ps1", bufs=3))
+        ps1 = ctx.enter_context(tc.psum_pool(name="ps1", bufs=4))
         ps2 = ctx.enter_context(tc.psum_pool(name="ps2", bufs=2))
         psd = ctx.enter_context(tc.psum_pool(name="psd", bufs=1))
         psm = ctx.enter_context(tc.psum_pool(name="psm", bufs=1))
@@ -62,7 +61,6 @@ def tile_maternkernel_t_kernel(tc, x1, x2, lengthscale, out):
         for i in range(2):
             nc.vector.quantize_mx(out=zc[:, 256 * i:256 * i + 256].bitcast(FP8X4),
                                   scales=zs[:, 256 * i:256 * i + 256], in_=zb[:])
-        pd = psd.tile([P, 4, NCH, RN], F32, name="pd", tag="pd")
         pi = psd.tile([P, 512], F32, name="pi", tag="pi")
 
         def idle0(n):
@@ -78,6 +76,8 @@ def tile_maternkernel_t_kernel(tc, x1, x2, lengthscale, out):
         nc.vector.memset(ones[:], 1.0)
         oneb = const.tile([P, RN], BF16, name="oneb")
         nc.vector.memset(oneb[:], 1.0)
+        epsq = const.tile([P, 1], F32, name="epsq")
+        nc.vector.memset(epsq[:], 1e-30)
         warm = const.tile([P, 1], F32, name="warm")
         nc.scalar.activation(out=warm[:], in_=ones[:, 0:1], func=ACT.Sqrt)
 
@@ -99,6 +99,8 @@ def tile_maternkernel_t_kernel(tc, x1, x2, lengthscale, out):
 
         xT = {}
         xn = {}
+        px1 = {}
+        pds = {}
 
         def load(q):
             h, c = q // NCH, q % NCH
@@ -128,20 +130,23 @@ def tile_maternkernel_t_kernel(tc, x1, x2, lengthscale, out):
                 nc.scalar.activation(out=xT[c][:, j, :], in_=pt[:], func=ACT.Copy,
                                      accum_out=sumsS[:, j - nv, c:c + 1])
 
-        def unit1(c, j):
-            q = NCH + c
-            if j == 0:
-                xT[q] = work.tile([P, 4, CW], BF16, name="xT", tag="xT", bufs=XTB)
-            pt = transposes(1, c, j)
-            if j in VJ:
-                nc.vector.tensor_copy(out=xT[q][:, j, :], in_=pt[:])
-            else:
-                nc.scalar.copy(out=xT[q][:, j, :], in_=pt[:])
+        def st_x(k):
+            g = k - NG
+            c = g // 2
+            px1[k] = []
+            for i in range(2):
+                pt = ps1.tile([P, 2, GW], BF16, name="pt", tag="pt")
+                for jj in range(2):
+                    j = 2 * i + jj
+                    for tl in range(4):
+                        nc.tensor.transpose(pt[:, jj, tl * P:(tl + 1) * P],
+                                            xn[NCH + c][:, 4 * (g % 2) + tl, j * P:(j + 1) * P], identb[:])
+                px1[k].append(pt)
 
         def row_sums1(c):
             for j in range(4):
                 for tt in range(CH):
-                    nc.tensor.matmul(out=pd[:, j, c, :], lhsT=xn[NCH + c][:, tt, j * P:(j + 1) * P], rhs=oneb[:],
+                    nc.tensor.matmul(out=pds[0][:, j, c, :], lhsT=xn[NCH + c][:, tt, j * P:(j + 1) * P], rhs=oneb[:],
                                      start=(tt == 0), stop=(tt == CH - 1))
 
         def mean_of(h):
@@ -151,7 +156,7 @@ def tile_maternkernel_t_kernel(tc, x1, x2, lengthscale, out):
                 nc.vector.tensor_reduce(out=msum[:, 0:nv], in_=sumsV[:], axis=AX.X, op=ALU.add)
                 nc.vector.tensor_reduce(out=msum[:, nv:4], in_=sumsS[:], axis=AX.X, op=ALU.add)
             else:
-                nc.vector.tensor_reduce(out=msum[:], in_=pd[:, :, :, 0],
+                nc.vector.tensor_reduce(out=msum[:], in_=pds[0][:, :, :, 0],
                                         axis=AX.X, op=ALU.add)
             nc.vector.tensor_scalar(out=mean[h][:], in0=msum[:], scalar1=1.0 / N1, scalar2=None, op0=ALU.mult)
             nc.vector.scalar_tensor_tensor(out=nbias[h][:], in0=mean[h][:], scalar=-1.0,
@@ -198,11 +203,16 @@ def tile_maternkernel_t_kernel(tc, x1, x2, lengthscale, out):
         sca = {}
         pm = {}
         wt = {}
+        s1g = {}
+        wb = {}
+        eb = {}
         et = {}
 
         def src_of(k, j):
-            h, g = k // NG, k % NG
-            return xT[h * NCH + g // 2][:, j, (g % 2) * GW:(g % 2 + 1) * GW]
+            g = k % NG
+            if k < NG:
+                return xT[g // 2][:, j, (g % 2) * GW:(g % 2 + 1) * GW]
+            return px1[k][j // 2][:, j % 2, :]
 
         def st_square(k):
             sq[k] = work.tile([P, 4, GW], F32, name="sq", tag="sq", bufs=3)
@@ -212,7 +222,11 @@ def tile_maternkernel_t_kernel(tc, x1, x2, lengthscale, out):
         def st_affine(k):
             ab[k] = work.tile([P, 4, GW], BF16, name="ab", tag="ab", bufs=2)
             for j in range(4):
-                affine(k // NG, j, ab[k][:, j, :], src_of(k, j))
+                if k >= NG and j in SJ:
+                    nc.scalar.activation(out=ab[k][:, j, :], in_=src_of(k, j), func=ACT.Identity,
+                                         bias=nbias[1][:, j:j + 1], scale=rls[:, 4 + j:5 + j])
+                else:
+                    affine(k // NG, j, ab[k][:, j, :], src_of(k, j))
 
         def st_group(k):
             gr[k] = work.tile([P, GW, 4], BF16, name="gr", tag="gr", bufs=2, align_bytes=64)
@@ -225,8 +239,8 @@ def tile_maternkernel_t_kernel(tc, x1, x2, lengthscale, out):
                 cod[k] = codes0[:, g * GW:(g + 1) * GW]
                 sca[k] = scales0[:, g * GW:(g + 1) * GW]
             else:
-                c1 = work.tile([P, GW], U32, name="c1", tag="c1", bufs=2, align_bytes=64)
-                s1 = work.tile([P, GW], U8, name="s1", tag="s1", bufs=2, align_bytes=64)
+                c1 = work.tile([P, GW], U32, name="c1", tag="c1", bufs=3, align_bytes=64)
+                s1 = work.tile([P, GW], U8, name="s1", tag="s1", bufs=3, align_bytes=64)
                 cod[k] = c1[:]
                 sca[k] = s1[:]
             nc.vector.quantize_mx(out=cod[k].bitcast(FP8X4), scales=sca[k],
@@ -263,28 +277,32 @@ def tile_maternkernel_t_kernel(tc, x1, x2, lengthscale, out):
                                         start=(h == 0), stop=(h == 1))
 
         def st_d2(g):
-            sq1g = work.tile([P, 4], F32, name="sq1g", tag="sq1g", bufs=3)
+            sq1g = work.tile([P, 4], F32, name="sq1g", tag="sq1g", bufs=4)
             nc.vector.tensor_tensor(out=sq1g[:], in0=sqp[0][:, 4 * g:4 * g + 4], in1=sqp[1][:, 4 * g:4 * g + 4],
                                     op=ALU.add)
-            wt[g] = work.tile([P, 4, P], F32, name="wt", tag="wt", bufs=6)
-            nc.vector.scalar_tensor_tensor(out=wt[g][:], in0=pm[g][:].rearrange("p (t n) -> p t n", n=P),
+            if g % 4 == 0:
+                wb[g // 4] = work.tile([P, 4, 4, P], F32, name="wb", tag="xT", bufs=XTB)
+                eb[g // 4] = work.tile([P, 4, 4, P], F32, name="eb", tag="xT", bufs=XTB)
+            wt[g] = wb[g // 4][:, g % 4, :, :]
+            et[g] = eb[g // 4][:, g % 4, :, :]
+            nc.vector.scalar_tensor_tensor(out=wt[g], in0=pm[g][:].rearrange("p (t n) -> p t n", n=P),
                                            scalar=-2.0, in1=sq2bc[:].unsqueeze(1).to_broadcast([P, 4, P]),
                                            op0=ALU.mult, op1=ALU.add)
-            for tl in range(4):
-                nc.vector.tensor_scalar(out=wt[g][:, tl, :], in0=wt[g][:, tl, :], scalar1=sq1g[:, tl:tl + 1],
-                                        scalar2=1e-30, op0=ALU.add, op1=ALU.max)
+            s1g[g] = sq1g
 
         def st_sqrt(g):
-            nc.scalar.activation(out=wt[g][:], in_=wt[g][:], func=ACT.Sqrt, scale=3.0)
+            for tl in range(4):
+                nc.scalar.activation(out=wb[g // 4][:, g % 4, tl, :], in_=wb[g // 4][:, g % 4, tl, :], func=ACT.Relu,
+                                     bias=s1g[g][:, tl:tl + 1])
+            nc.scalar.activation(out=wt[g], in_=wt[g], func=ACT.Sqrt, scale=3.0, bias=epsq[:])
 
         def st_exp(g):
-            et[g] = work.tile([P, 4, P], F32, name="et", tag="et", bufs=3)
-            nc.scalar.activation(out=et[g][:], in_=wt[g][:], func=ACT.Exp, scale=-1.0)
+            nc.scalar.activation(out=et[g], in_=wt[g], func=ACT.Exp, scale=-1.0)
 
         def st_out(g):
-            nc.vector.scalar_tensor_tensor(out=et[g][:], in0=wt[g][:], scalar=1.0, in1=et[g][:],
+            nc.vector.scalar_tensor_tensor(out=et[g], in0=wt[g], scalar=1.0, in1=et[g],
                                            op0=ALU.add, op1=ALU.mult)
-            nc.sync.dma_start(out=outv[:, 4 * g:4 * g + 4, :], in_=et[g][:])
+            nc.sync.dma_start(out=outv[:, 4 * g:4 * g + 4, :], in_=et[g])
 
         batch_of = {}
         g0 = 0
@@ -315,28 +333,18 @@ def tile_maternkernel_t_kernel(tc, x1, x2, lengthscale, out):
                                 rhs=zc[:].bitcast(FP8X4), rhs_scale=zs[:], start=True, stop=True)
 
         pending = []
-        for s in range(2 * NG + 8):
-            c2 = s // 2 - LAG
-            if 0 <= c2 < NCH:
-                unit1(c2, 2 * (s % 2))
-                unit1(c2, 2 * (s % 2) + 1)
-                idle(max(0, s - 2), IDLET)
-                if s % 2 == 1 and NCH + c2 + XNB < 2 * NCH:
-                    load(NCH + c2 + XNB)
-            if s < XNB:
+        for s in range(2 * NG + 9):
+            if s == 0:
+                pds[0] = psm.tile([P, 4, NCH, RN], F32, name="pd", tag="pm")
+            if s < NCH:
                 row_sums1(s)
-            if XNB <= s // 2 - LAG + XNB - 1 < NCH and s % 2 == 1:
-                row_sums1(s // 2 - LAG + XNB - 1)
-            if s == 2 * MEAN1:
+            if s == NCH:
                 mean_of(1)
                 bpost(1)
                 sq2_spread()
-            if 0 <= s - 1 < 2 * NG:
-                st_quant(s - 1)
-                st_t2(s - 1)
             todo = pending
             pending = []
-            gs = s - NG - 4
+            gs = s - NG - 5
             if 0 <= gs < NG:
                 st_sqrt(gs)
                 if gs in batch_of:
@@ -346,6 +354,12 @@ def tile_maternkernel_t_kernel(tc, x1, x2, lengthscale, out):
             if s < 2 * NG:
                 st_square(s)
                 st_affine(s)
+            if 0 <= s - 1 < 2 * NG:
+                st_quant(s - 1)
+                st_t2(s - 1)
+            if NG <= s + AHEAD < 2 * NG:
+                st_x(s + AHEAD)
+                idle(s - 1, IDLET)
             if 0 <= s - 2 < 2 * NG:
                 st_red(s - 2)
             if s < 2 * NG:

@@ -5,17 +5,17 @@ from concourse.masks import make_identity
 
 FLOPS = 2 * 8192 * 128 * 1024
 
-BATCH = (7, 6, 3)
+BATCH = (8, 6, 2)
+PACE = 3
 E1S = 1
-SJ = ()
 XNB = 8
 XTB = 8
 AHEAD = 2
 WARM = 6
-BURST = 4
-IDLE = (3, 1)
-IDLET = 2
-RN = 16
+HEAD = 1
+BURST = 14
+RN = 4
+SR = 2
 
 FP8X4 = mybir.dt.float8_e4m3fn_x4
 BF16 = mybir.dt.bfloat16
@@ -68,6 +68,10 @@ def tile_maternkernel_t_kernel(tc, x1, x2, lengthscale, out):
                 nc.tensor.matmul_mx(out=pi[:], lhsT=zc[:, 0:P].bitcast(FP8X4), lhsT_scale=zs[:, 0:P],
                                     rhs=zc[:].bitcast(FP8X4), rhs_scale=zs[:], start=True, stop=True)
 
+        def idle1(n):
+            for i in range(n):
+                nc.tensor.matmul(out=pi[:, 0:P], lhsT=identf[:], rhs=identf[:], start=True, stop=True)
+
         identb = const.tile([P, P], BF16, name="identb")
         make_identity(nc, identb[:])
         identf = const.tile([P, P], F32, name="identf")
@@ -111,11 +115,7 @@ def tile_maternkernel_t_kernel(tc, x1, x2, lengthscale, out):
             q = h * NCH + c
             pt = ps1.tile([P, CW], BF16, name="pt", tag="pt")
             for tt in range(CH):
-                src = xn[q][:, tt, j * P:(j + 1) * P]
-                if h == 0 and tt == 7 and j % 2 == 1:
-                    nc.tensor.matmul(out=pt[:, tt * P:(tt + 1) * P], lhsT=src, rhs=identb[:], start=True, stop=True)
-                else:
-                    nc.tensor.transpose(pt[:, tt * P:(tt + 1) * P], src, identb[:])
+                nc.tensor.transpose(pt[:, tt * P:(tt + 1) * P], xn[q][:, tt, j * P:(j + 1) * P], identb[:])
             return pt
 
         def unit0(c, j):
@@ -142,6 +142,8 @@ def tile_maternkernel_t_kernel(tc, x1, x2, lengthscale, out):
                         nc.tensor.transpose(pt[:, jj, tl * P:(tl + 1) * P],
                                             xn[NCH + c][:, 4 * (g % 2) + tl, j * P:(j + 1) * P], identb[:])
                 px1[k].append(pt)
+                if i == 0:
+                    idle0(1)
 
         def row_sums1(c):
             for j in range(4):
@@ -172,7 +174,7 @@ def tile_maternkernel_t_kernel(tc, x1, x2, lengthscale, out):
 
         def bpost(h):
             abb = const.tile([P, 4, P], BF16, name="abb", tag="abb", bufs=1)
-            sqb = const.tile([P, 4, P], F32, name="sqb", tag="sqb", bufs=1)
+            sqb = const.tile([P, 4, P], F32, name="sqb", tag="sqb", bufs=2)
             for j in range(4):
                 square(h, j, sqb[:, j, :], x2T[:, 4 * h + j, :])
                 affine(h, j, abb[:, j, :], x2T[:, 4 * h + j, :])
@@ -180,6 +182,9 @@ def tile_maternkernel_t_kernel(tc, x1, x2, lengthscale, out):
             nc.vector.tensor_copy(out=grb[:], in_=abb[:].rearrange("p j r -> p r j"))
             nc.vector.quantize_mx(out=bcodes[h][:].bitcast(FP8X4), scales=bscales[h][:],
                                   in_=grb[:].rearrange("p r j -> p (r j)"))
+            return sqb
+
+        def bsum(h, sqb):
             pb = psm.tile([P, 512], F32, name="pb", tag="pm")
             for j in range(4):
                 nc.tensor.matmul(out=pb[:, 0:P], lhsT=sqb[:, j, :], rhs=identf[:], is_transpose=True,
@@ -222,11 +227,7 @@ def tile_maternkernel_t_kernel(tc, x1, x2, lengthscale, out):
         def st_affine(k):
             ab[k] = work.tile([P, 4, GW], BF16, name="ab", tag="ab", bufs=2)
             for j in range(4):
-                if k >= NG and j in SJ:
-                    nc.scalar.activation(out=ab[k][:, j, :], in_=src_of(k, j), func=ACT.Identity,
-                                         bias=nbias[1][:, j:j + 1], scale=rls[:, 4 + j:5 + j])
-                else:
-                    affine(k // NG, j, ab[k][:, j, :], src_of(k, j))
+                affine(k // NG, j, ab[k][:, j, :], src_of(k, j))
 
         def st_group(k):
             gr[k] = work.tile([P, GW, 4], BF16, name="gr", tag="gr", bufs=2, align_bytes=64)
@@ -246,19 +247,18 @@ def tile_maternkernel_t_kernel(tc, x1, x2, lengthscale, out):
             nc.vector.quantize_mx(out=cod[k].bitcast(FP8X4), scales=sca[k],
                                   in_=gr[k][:].rearrange("p r j -> p (r j)"))
 
-        def idle(k, n):
-            h = k // NG
-            for i in range(n):
-                nc.tensor.matmul_mx(out=pi[:], lhsT=bcodes[h][:].bitcast(FP8X4), lhsT_scale=bscales[h][:],
-                                    rhs=cod[k].bitcast(FP8X4), rhs_scale=sca[k], start=True, stop=True)
-
         def st_t2(k):
             pa[k] = ps2.tile([P, 512], F32, name="pa", tag="pa")
             for tl in range(4):
                 for j in range(4):
                     nc.tensor.matmul(out=pa[k][:, tl * P:(tl + 1) * P], lhsT=sq[k][:, j, tl * P:(tl + 1) * P],
                                      rhs=identf[:], is_transpose=True, start=(j == 0), stop=(j == 3))
-            idle(k, IDLE[k // NG])
+                if tl == 1 and k < NG:
+                    idle1(1)
+                elif tl == 1:
+                    idle0(1)
+            if k < NG:
+                idle1(1)
 
         def st_red(k):
             h, g = k // NG, k % NG
@@ -277,8 +277,8 @@ def tile_maternkernel_t_kernel(tc, x1, x2, lengthscale, out):
                                         start=(h == 0), stop=(h == 1))
 
         def st_d2(g):
-            sq1g = work.tile([P, 4], F32, name="sq1g", tag="sq1g", bufs=4)
-            nc.vector.tensor_tensor(out=sq1g[:], in0=sqp[0][:, 4 * g:4 * g + 4], in1=sqp[1][:, 4 * g:4 * g + 4],
+            s1g[g] = work.tile([P, 4], F32, name="sq1g", tag="sq1g", bufs=4)
+            nc.gpsimd.tensor_tensor(out=s1g[g][:], in0=sqp[0][:, 4 * g:4 * g + 4], in1=sqp[1][:, 4 * g:4 * g + 4],
                                     op=ALU.add)
             if g % 4 == 0:
                 wb[g // 4] = work.tile([P, 4, 4, P], F32, name="wb", tag="xT", bufs=XTB)
@@ -288,10 +288,14 @@ def tile_maternkernel_t_kernel(tc, x1, x2, lengthscale, out):
             nc.vector.scalar_tensor_tensor(out=wt[g], in0=pm[g][:].rearrange("p (t n) -> p t n", n=P),
                                            scalar=-2.0, in1=sq2bc[:].unsqueeze(1).to_broadcast([P, 4, P]),
                                            op0=ALU.mult, op1=ALU.add)
-            s1g[g] = sq1g
+
+        def st_clamp(g):
+            for tl in range(4 - SR):
+                w = wb[g // 4][:, g % 4, tl, :]
+                nc.vector.tensor_scalar(out=w, in0=w, scalar1=s1g[g][:, tl:tl + 1], scalar2=0.0, op0=ALU.add, op1=ALU.max)
 
         def st_sqrt(g):
-            for tl in range(4):
+            for tl in range(4 - SR, 4):
                 nc.scalar.activation(out=wb[g // 4][:, g % 4, tl, :], in_=wb[g // 4][:, g % 4, tl, :], func=ACT.Relu,
                                      bias=s1g[g][:, tl:tl + 1])
             nc.scalar.activation(out=wt[g], in_=wt[g], func=ACT.Sqrt, scale=3.0, bias=epsq[:])
@@ -304,18 +308,22 @@ def tile_maternkernel_t_kernel(tc, x1, x2, lengthscale, out):
                                            op0=ALU.add, op1=ALU.mult)
             nc.sync.dma_start(out=outv[:, 4 * g:4 * g + 4, :], in_=et[g])
 
-        batch_of = {}
+        tasks = []
         g0 = 0
         for b in BATCH:
-            batch_of[g0 + b - 1] = list(range(g0, g0 + b))
+            tasks.extend([("sqrt", g) for g in range(g0, g0 + b)])
+            tasks.extend([("exp", g) for g in range(g0, g0 + b)])
             g0 += b
+        sqbs = []
 
         for q in range(XNB):
             load(q)
+        ctx.enter_context(tc.manual_schedule(engines={mybir.EngineType.PE, mybir.EngineType.Activation}))
         idle0(WARM)
         for c in range(NCH):
             for j in range(4):
                 unit0(c, j)
+            idle1(HEAD)
             load(c + XNB)
             if c == 2:
                 pl = ps1.tile([P, CW], BF16, name="pl", tag="pt")
@@ -326,47 +334,51 @@ def tile_maternkernel_t_kernel(tc, x1, x2, lengthscale, out):
                 for kt in range(8):
                     nc.tensor.transpose(px[:, kt * P:(kt + 1) * P], x2n[:, kt * P:(kt + 1) * P], identb[:])
                 nc.vector.tensor_copy(out=x2T[:].rearrange("p k n -> p (k n)"), in_=px[:])
+        idle0(BURST)
         mean_of(0)
-        bpost(0)
-        for i in range(BURST):
-            nc.tensor.matmul_mx(out=pi[:], lhsT=bcodes[0][:].bitcast(FP8X4), lhsT_scale=bscales[0][:],
-                                rhs=zc[:].bitcast(FP8X4), rhs_scale=zs[:], start=True, stop=True)
 
         pending = []
-        for s in range(2 * NG + 9):
+        for s in range(2 * NG + 10):
             if s == 0:
                 pds[0] = psm.tile([P, 4, NCH, RN], F32, name="pd", tag="pm")
             if s < NCH:
                 row_sums1(s)
             if s == NCH:
                 mean_of(1)
-                bpost(1)
+            if NCH <= s < NCH + 2:
+                sqbs.append(bpost(s - NCH))
+            if NCH + 2 <= s < NCH + 4:
+                bsum(s - NCH - 2, sqbs[s - NCH - 2])
+            if s == NCH + 5:
                 sq2_spread()
             todo = pending
             pending = []
-            gs = s - NG - 5
-            if 0 <= gs < NG:
-                st_sqrt(gs)
-                if gs in batch_of:
-                    for g in batch_of[gs]:
+            for i in range(PACE):
+                if tasks and (tasks[0][0] == "exp" or tasks[0][1] <= s - NG - 5):
+                    kind, g = tasks[0]
+                    tasks = tasks[1:]
+                    if kind == "sqrt":
+                        st_sqrt(g)
+                    else:
                         st_exp(g)
-                    pending = batch_of[gs]
+                        pending.append(g)
             if s < 2 * NG:
                 st_square(s)
                 st_affine(s)
             if 0 <= s - 1 < 2 * NG:
                 st_quant(s - 1)
                 st_t2(s - 1)
-            if NG <= s + AHEAD < 2 * NG:
-                st_x(s + AHEAD)
-                idle(s - 1, IDLET)
-            if 0 <= s - 2 < 2 * NG:
-                st_red(s - 2)
-            if s < 2 * NG:
-                st_group(s)
             if 0 <= s - NG - 2 < NG:
                 st_mx(s - NG - 2)
+            if NG <= s + AHEAD < 2 * NG:
+                st_x(s + AHEAD)
             if 0 <= s - NG - 3 < NG:
                 st_d2(s - NG - 3)
+            if 0 <= s - 2 < 2 * NG:
+                st_red(s - 2)
+            if 0 <= s - NG - 3 < NG:
+                st_clamp(s - NG - 3)
+            if s < 2 * NG:
+                st_group(s)
             for g in todo:
                 st_out(g)

from contextlib import ExitStack

import concourse.mybir as mybir
from concourse.masks import make_identity

FLOPS = 2 * 8192 * 128 * 1024

BATCH = (8, 6, 2)
PACE = 3
E1S = 1
XNB = 8
XTB = 8
AHEAD = 2
WARM = 6
HEAD = 1
BURST = 14
RN = 4
SR = 2

FP8X4 = mybir.dt.float8_e4m3fn_x4
BF16 = mybir.dt.bfloat16
F32 = mybir.dt.float32
U32 = mybir.dt.uint32
U8 = mybir.dt.uint8
ALU = mybir.AluOpType
ACT = mybir.ActivationFunctionType
AX = mybir.AxisListType

P = 128
N1 = 8192
D = 1024
NT = N1 // P
CH = 8
NCH = NT // CH
CW = CH * P
GW = 512
NG = N1 // GW


def tile_maternkernel_t_kernel(tc, x1, x2, lengthscale, out):
    nc = tc.nc
    x1v = x1.rearrange("(p t) f -> p t f", t=NT)
    outv = out.rearrange("(p t) n -> p t n", t=NT)
    with ExitStack() as ctx:
        const = ctx.enter_context(tc.tile_pool(name="const", bufs=1))
        work = ctx.enter_context(tc.tile_pool(name="work", bufs=2))
        ps1 = ctx.enter_context(tc.psum_pool(name="ps1", bufs=4))
        ps2 = ctx.enter_context(tc.psum_pool(name="ps2", bufs=2))
        psd = ctx.enter_context(tc.psum_pool(name="psd", bufs=1))
        psm = ctx.enter_context(tc.psum_pool(name="psm", bufs=1))

        lsz = const.tile([P, P], BF16, name="lsz")
        nc.vector.memset(lsz[:], 0.0)
        nc.scalar.dma_start(out=lsz[0:8, :], in_=lengthscale.rearrange("(k p) -> k p", p=P))
        x2n = const.tile([P, D], BF16, name="x2n")
        nc.scalar.dma_start(out=x2n[:], in_=x2)
        zb = const.tile([P, 1024], BF16, name="zb", align_bytes=64)
        nc.vector.memset(zb[:], 1.0)
        zc = const.tile([P, 512], U32, name="zc", align_bytes=64)
        zs = const.tile([P, 512], U8, name="zs", align_bytes=64)
        for i in range(2):
            nc.vector.quantize_mx(out=zc[:, 256 * i:256 * i + 256].bitcast(FP8X4),
                                  scales=zs[:, 256 * i:256 * i + 256], in_=zb[:])
        pi = psd.tile([P, 512], F32, name="pi", tag="pi")

        def idle0(n):
            for i in range(n):
                nc.tensor.matmul_mx(out=pi[:], lhsT=zc[:, 0:P].bitcast(FP8X4), lhsT_scale=zs[:, 0:P],
                                    rhs=zc[:].bitcast(FP8X4), rhs_scale=zs[:], start=True, stop=True)

        def idle1(n):
            for i in range(n):
                nc.tensor.matmul(out=pi[:, 0:P], lhsT=identf[:], rhs=identf[:], start=True, stop=True)

        identb = const.tile([P, P], BF16, name="identb")
        make_identity(nc, identb[:])
        identf = const.tile([P, P], F32, name="identf")
        make_identity(nc, identf[:])
        ones = const.tile([P, P], F32, name="ones")
        nc.vector.memset(ones[:], 1.0)
        oneb = const.tile([P, RN], BF16, name="oneb")
        nc.vector.memset(oneb[:], 1.0)
        epsq = const.tile([P, 1], F32, name="epsq")
        nc.vector.memset(epsq[:], 1e-30)
        warm = const.tile([P, 1], F32, name="warm")
        nc.scalar.activation(out=warm[:], in_=ones[:, 0:1], func=ACT.Sqrt)

        lsT = const.tile([P, 8], F32, name="lsT")
        rls = const.tile([P, 8], F32, name="rls")
        x2T = const.tile([P, 8, P], BF16, name="x2T")

        codes0 = const.tile([P, N1], U32, name="codes0", align_bytes=64)
        scales0 = const.tile([P, N1], U8, name="scales0", align_bytes=64)
        bcodes = [const.tile([P, P], U32, name="bcodes%d" % h, align_bytes=64) for h in range(2)]
        bscales = [const.tile([P, P], U8, name="bscales%d" % h, align_bytes=64) for h in range(2)]
        sqp = [const.tile([P, NT], F32, name="sqp%d" % h) for h in range(2)]
        sq2p = const.tile([P, 2], F32, name="sq2p")
        sq2bc = const.tile([P, P], F32, name="sq2bc")
        sumsV = const.tile([P, 4 - E1S, NCH], F32, name="sumsV")
        sumsS = const.tile([P, E1S, NCH], F32, name="sumsS")
        mean = [const.tile([P, 4], F32, name="mean%d" % h) for h in range(2)]
        nbias = [const.tile([P, 4], F32, name="nbias%d" % h) for h in range(2)]

        xT = {}
        xn = {}
        px1 = {}
        pds = {}

        def load(q):
            h, c = q // NCH, q % NCH
            xn[q] = work.tile([P, CH, 512], BF16, name="xn", tag="xn", bufs=XNB)
            nc.sync.dma_start(out=xn[q][:], in_=x1v[:, c * CH:(c + 1) * CH, h * 512:(h + 1) * 512])

        def transposes(h, c, j):
            q = h * NCH + c
            pt = ps1.tile([P, CW], BF16, name="pt", tag="pt")
            for tt in range(CH):
                nc.tensor.transpose(pt[:, tt * P:(tt + 1) * P], xn[q][:, tt, j * P:(j + 1) * P], identb[:])
            return pt

        def unit0(c, j):
            if j == 0:
                xT[c] = work.tile([P, 4, CW], BF16, name="xT", tag="xT", bufs=XTB)
            pt = transposes(0, c, j)
            nv = 4 - E1S
            if j < nv:
                nc.vector.tensor_scalar(out=xT[c][:, j, :], in0=pt[:], scalar1=1.0, scalar2=None,
                                        op0=ALU.mult, op1=ALU.add, accum_out=sumsV[:, j, c:c + 1])
            else:
                nc.scalar.activation(out=xT[c][:, j, :], in_=pt[:], func=ACT.Copy,
                                     accum_out=sumsS[:, j - nv, c:c + 1])

        def st_x(k):
            g = k - NG
            c = g // 2
            px1[k] = []
            for i in range(2):
                pt = ps1.tile([P, 2, GW], BF16, name="pt", tag="pt")
                for jj in range(2):
                    j = 2 * i + jj
                    for tl in range(4):
                        nc.tensor.transpose(pt[:, jj, tl * P:(tl + 1) * P],
                                            xn[NCH + c][:, 4 * (g % 2) + tl, j * P:(j + 1) * P], identb[:])
                px1[k].append(pt)
                if i == 0:
                    idle0(1)

        def row_sums1(c):
            for j in range(4):
                for tt in range(CH):
                    nc.tensor.matmul(out=pds[0][:, j, c, :], lhsT=xn[NCH + c][:, tt, j * P:(j + 1) * P], rhs=oneb[:],
                                     start=(tt == 0), stop=(tt == CH - 1))

        def mean_of(h):
            msum = const.tile([P, 4], F32, name="msum%d" % h)
            if h == 0:
                nv = 4 - E1S
                nc.vector.tensor_reduce(out=msum[:, 0:nv], in_=sumsV[:], axis=AX.X, op=ALU.add)
                nc.vector.tensor_reduce(out=msum[:, nv:4], in_=sumsS[:], axis=AX.X, op=ALU.add)
            else:
                nc.vector.tensor_reduce(out=msum[:], in_=pds[0][:, :, :, 0],
                                        axis=AX.X, op=ALU.add)
            nc.vector.tensor_scalar(out=mean[h][:], in0=msum[:], scalar1=1.0 / N1, scalar2=None, op0=ALU.mult)
            nc.vector.scalar_tensor_tensor(out=nbias[h][:], in0=mean[h][:], scalar=-1.0,
                                           in1=rls[:, 4 * h:4 * h + 4], op0=ALU.mult, op1=ALU.mult)

        def affine(h, j, dst, src):
            nc.vector.tensor_scalar(out=dst, in0=src, scalar1=mean[h][:, j:j + 1],
                                    scalar2=rls[:, 4 * h + j:4 * h + j + 1], op0=ALU.subtract, op1=ALU.mult)

        def square(h, j, dst, src):
            nc.scalar.activation(out=dst, in_=src, func=ACT.Square, bias=nbias[h][:, j:j + 1],
                                 scale=rls[:, 4 * h + j:4 * h + j + 1])

        def bpost(h):
            abb = const.tile([P, 4, P], BF16, name="abb", tag="abb", bufs=1)
            sqb = const.tile([P, 4, P], F32, name="sqb", tag="sqb", bufs=2)
            for j in range(4):
                square(h, j, sqb[:, j, :], x2T[:, 4 * h + j, :])
                affine(h, j, abb[:, j, :], x2T[:, 4 * h + j, :])
            grb = const.tile([P, P, 4], BF16, name="grb", tag="grb", bufs=1, align_bytes=64)
            nc.vector.tensor_copy(out=grb[:], in_=abb[:].rearrange("p j r -> p r j"))
            nc.vector.quantize_mx(out=bcodes[h][:].bitcast(FP8X4), scales=bscales[h][:],
                                  in_=grb[:].rearrange("p r j -> p (r j)"))
            return sqb

        def bsum(h, sqb):
            pb = psm.tile([P, 512], F32, name="pb", tag="pm")
            for j in range(4):
                nc.tensor.matmul(out=pb[:, 0:P], lhsT=sqb[:, j, :], rhs=identf[:], is_transpose=True,
                                 start=(j == 0), stop=(j == 3))
            nc.vector.tensor_reduce(out=sq2p[:, h:h + 1], in_=pb[:, 0:P], axis=AX.X, op=ALU.add)

        def sq2_spread():
            sq2 = const.tile([P, 1], F32, name="sq2")
            nc.vector.tensor_reduce(out=sq2[:], in_=sq2p[:], axis=AX.X, op=ALU.add)
            rep = const.tile([P, P], F32, name="rep")
            nc.vector.tensor_scalar(out=rep[:], in0=ones[:], scalar1=sq2[:, 0:1], scalar2=None, op0=ALU.mult)
            pr = psm.tile([P, 512], F32, name="pr", tag="pm")
            nc.tensor.transpose(pr[:, 0:P], rep[:], identf[:])
            nc.vector.tensor_copy(out=sq2bc[:], in_=pr[:, 0:P])

        sq = {}
        ab = {}
        gr = {}
        pa = {}
        cod = {}
        sca = {}
        pm = {}
        wt = {}
        s1g = {}
        wb = {}
        eb = {}
        et = {}

        def src_of(k, j):
            g = k % NG
            if k < NG:
                return xT[g // 2][:, j, (g % 2) * GW:(g % 2 + 1) * GW]
            return px1[k][j // 2][:, j % 2, :]

        def st_square(k):
            sq[k] = work.tile([P, 4, GW], F32, name="sq", tag="sq", bufs=3)
            for j in range(4):
                square(k // NG, j, sq[k][:, j, :], src_of(k, j))

        def st_affine(k):
            ab[k] = work.tile([P, 4, GW], BF16, name="ab", tag="ab", bufs=2)
            for j in range(4):
                affine(k // NG, j, ab[k][:, j, :], src_of(k, j))

        def st_group(k):
            gr[k] = work.tile([P, GW, 4], BF16, name="gr", tag="gr", bufs=2, align_bytes=64)
            nc.vector.tensor_copy(out=gr[k][:].rearrange("p (c i) t -> p c t i", i=4),
                                  in_=ab[k][:].rearrange("p t (c i) -> p c t i", i=4))

        def st_quant(k):
            h, g = k // NG, k % NG
            if h == 0:
                cod[k] = codes0[:, g * GW:(g + 1) * GW]
                sca[k] = scales0[:, g * GW:(g + 1) * GW]
            else:
                c1 = work.tile([P, GW], U32, name="c1", tag="c1", bufs=3, align_bytes=64)
                s1 = work.tile([P, GW], U8, name="s1", tag="s1", bufs=3, align_bytes=64)
                cod[k] = c1[:]
                sca[k] = s1[:]
            nc.vector.quantize_mx(out=cod[k].bitcast(FP8X4), scales=sca[k],
                                  in_=gr[k][:].rearrange("p r j -> p (r j)"))

        def st_t2(k):
            pa[k] = ps2.tile([P, 512], F32, name="pa", tag="pa")
            for tl in range(4):
                for j in range(4):
                    nc.tensor.matmul(out=pa[k][:, tl * P:(tl + 1) * P], lhsT=sq[k][:, j, tl * P:(tl + 1) * P],
                                     rhs=identf[:], is_transpose=True, start=(j == 0), stop=(j == 3))
                if tl == 1 and k < NG:
                    idle1(1)
                elif tl == 1:
                    idle0(1)
            if k < NG:
                idle1(1)

        def st_red(k):
            h, g = k // NG, k % NG
            nc.vector.tensor_reduce(out=sqp[h][:, 4 * g:4 * g + 4],
                                    in_=pa[k][:].rearrange("p (t n) -> p t n", n=P), axis=AX.X, op=ALU.add)

        def st_mx(g):
            pm[g] = psm.tile([P, 512], F32, name="pm", tag="pm")
            for tl in range(4):
                for h in range(2):
                    k = h * NG + g
                    nc.tensor.matmul_mx(out=pm[g][:, tl * P:(tl + 1) * P],
                                        lhsT=cod[k][:, tl * P:(tl + 1) * P].bitcast(FP8X4),
                                        lhsT_scale=sca[k][:, tl * P:(tl + 1) * P],
                                        rhs=bcodes[h][:].bitcast(FP8X4), rhs_scale=bscales[h][:],
                                        start=(h == 0), stop=(h == 1))

        def st_d2(g):
            s1g[g] = work.tile([P, 4], F32, name="sq1g", tag="sq1g", bufs=4)
            nc.gpsimd.tensor_tensor(out=s1g[g][:], in0=sqp[0][:, 4 * g:4 * g + 4], in1=sqp[1][:, 4 * g:4 * g + 4],
                                    op=ALU.add)
            if g % 4 == 0:
                wb[g // 4] = work.tile([P, 4, 4, P], F32, name="wb", tag="xT", bufs=XTB)
                eb[g // 4] = work.tile([P, 4, 4, P], F32, name="eb", tag="xT", bufs=XTB)
            wt[g] = wb[g // 4][:, g % 4, :, :]
            et[g] = eb[g // 4][:, g % 4, :, :]
            nc.vector.scalar_tensor_tensor(out=wt[g], in0=pm[g][:].rearrange("p (t n) -> p t n", n=P),
                                           scalar=-2.0, in1=sq2bc[:].unsqueeze(1).to_broadcast([P, 4, P]),
                                           op0=ALU.mult, op1=ALU.add)

        def st_clamp(g):
            for tl in range(4 - SR):
                w = wb[g // 4][:, g % 4, tl, :]
                nc.vector.tensor_scalar(out=w, in0=w, scalar1=s1g[g][:, tl:tl + 1], scalar2=0.0, op0=ALU.add, op1=ALU.max)

        def st_sqrt(g):
            for tl in range(4 - SR, 4):
                nc.scalar.activation(out=wb[g // 4][:, g % 4, tl, :], in_=wb[g // 4][:, g % 4, tl, :], func=ACT.Relu,
                                     bias=s1g[g][:, tl:tl + 1])
            nc.scalar.activation(out=wt[g], in_=wt[g], func=ACT.Sqrt, scale=3.0, bias=epsq[:])

        def st_exp(g):
            nc.scalar.activation(out=et[g], in_=wt[g], func=ACT.Exp, scale=-1.0)

        def st_out(g):
            nc.vector.scalar_tensor_tensor(out=et[g], in0=wt[g], scalar=1.0, in1=et[g],
                                           op0=ALU.add, op1=ALU.mult)
            nc.sync.dma_start(out=outv[:, 4 * g:4 * g + 4, :], in_=et[g])

        tasks = []
        g0 = 0
        for b in BATCH:
            tasks.extend([("sqrt", g) for g in range(g0, g0 + b)])
            tasks.extend([("exp", g) for g in range(g0, g0 + b)])
            g0 += b
        sqbs = []

        for q in range(XNB):
            load(q)
        ctx.enter_context(tc.manual_schedule(engines={mybir.EngineType.PE, mybir.EngineType.Activation}))
        idle0(WARM)
        for c in range(NCH):
            for j in range(4):
                unit0(c, j)
            idle1(HEAD)
            load(c + XNB)
            if c == 2:
                pl = ps1.tile([P, CW], BF16, name="pl", tag="pt")
                nc.tensor.transpose(pl[:, 0:P], lsz[:], identb[:])
                nc.vector.tensor_copy(out=lsT[:], in_=pl[:, 0:8])
                nc.vector.reciprocal(out=rls[:], in_=lsT[:])
                px = ps1.tile([P, CW], BF16, name="px", tag="pt")
                for kt in range(8):
                    nc.tensor.transpose(px[:, kt * P:(kt + 1) * P], x2n[:, kt * P:(kt + 1) * P], identb[:])
                nc.vector.tensor_copy(out=x2T[:].rearrange("p k n -> p (k n)"), in_=px[:])
        idle0(BURST)
        mean_of(0)

        pending = []
        for s in range(2 * NG + 10):
            if s == 0:
                pds[0] = psm.tile([P, 4, NCH, RN], F32, name="pd", tag="pm")
            if s < NCH:
                row_sums1(s)
            if s == NCH:
                mean_of(1)
            if NCH <= s < NCH + 2:
                sqbs.append(bpost(s - NCH))
            if NCH + 2 <= s < NCH + 4:
                bsum(s - NCH - 2, sqbs[s - NCH - 2])
            if s == NCH + 5:
                sq2_spread()
            todo = pending
            pending = []
            for i in range(PACE):
                if tasks and (tasks[0][0] == "exp" or tasks[0][1] <= s - NG - 5):
                    kind, g = tasks[0]
                    tasks = tasks[1:]
                    if kind == "sqrt":
                        st_sqrt(g)
                    else:
                        st_exp(g)
                        pending.append(g)
            if s < 2 * NG:
                st_square(s)
                st_affine(s)
            if 0 <= s - 1 < 2 * NG:
                st_quant(s - 1)
                st_t2(s - 1)
            if 0 <= s - NG - 2 < NG:
                st_mx(s - NG - 2)
            if NG <= s + AHEAD < 2 * NG:
                st_x(s + AHEAD)
            if 0 <= s - NG - 3 < NG:
                st_d2(s - NG - 3)
            if 0 <= s - 2 < 2 * NG:
                st_red(s - 2)
            if 0 <= s - NG - 3 < NG:
                st_clamp(s - NG - 3)
            if s < 2 * NG:
                st_group(s)
            for g in todo:
                st_out(g)
